import numpy as np
import ml_dtypes


def mxq(x, axis, fmt="e4m3"):
    dtype, down = {"e4m3": (ml_dtypes.float8_e4m3fn, 7), "e5m2": (ml_dtypes.float8_e5m2, 14)}[fmt]
    v = np.moveaxis(np.asarray(x, np.float32).astype(ml_dtypes.bfloat16).astype(np.float64), axis, -1)
    blocks = v.reshape(v.shape[:-1] + (-1, 32))
    amax = np.abs(blocks).max(-1, keepdims=True)
    byte = np.maximum(np.where(amax > 0, np.frexp(amax)[1] - 1 + 127, 0) - down, 1)
    scale = np.exp2(byte - 127.0)
    codes = (blocks / scale).astype(np.float32).astype(dtype).astype(np.float64)
    return np.moveaxis((codes * scale).reshape(v.shape), -1, axis)


WIDE = False


def mx_kscale(k):
    if not WIDE:
        return np.ones(k)
    levels = np.array([10, -10, 5, -5, 0])
    a = np.random.permutation(np.resize(levels, k // 512 * 4)).reshape(k // 512, 4)
    idx = np.arange(k)
    return np.exp2(a[idx // 512, idx % 128 // 32])


BF16 = ml_dtypes.bfloat16


def bf(x):
    return np.asarray(x, np.float32).astype(BF16)


def f64(x):
    return np.asarray(x).astype(np.float64)


E2M1 = np.array([0.0, 0.5, 1.0, 1.5, 2.0, 3.0, 4.0, 6.0, -0.0, -0.5, -1.0, -1.5, -2.0, -3.0, -4.0, -6.0])


def pack_weight(w, fmt):
    k, n = w.shape
    w = f64(bf(w)).reshape(k // 32, 32, n)
    amax = np.abs(w).max(1)
    if fmt == "e4m3":
        byte = np.frexp(amax)[1] - 1 + 127 - 7
    else:
        mant, ex = np.frexp(amax / 6.0)
        byte = np.where(mant > 0.5, ex, ex - 1) + 127
    byte = np.clip(np.where(amax > 0, byte, 1), 1, 254)
    scaled = (w * np.exp2(127.0 - byte)[:, None, :]).reshape(k, n).astype(np.float32)
    by_word = np.ascontiguousarray(scaled.reshape(k // 512, 128, 4, n).transpose(0, 1, 3, 2))
    if fmt == "e4m3":
        words = by_word.astype(ml_dtypes.float8_e4m3fn).view(np.uint8)
    else:
        c = by_word.astype(ml_dtypes.float4_e2m1fn).view(np.uint8) & 0xF
        words = c[..., 0::2] | (c[..., 1::2] << 4)
    return np.ascontiguousarray(words), np.ascontiguousarray(byte.astype(np.uint8).reshape(k // 512, 16, n))


def unpack_weight(words, scales, fmt):
    g, p, n, _ = words.shape
    if fmt == "e4m3":
        vals = np.ascontiguousarray(words).view(ml_dtypes.float8_e4m3fn).astype(np.float64)
    else:
        nib = np.empty((g, p, n, 4), np.uint8)
        nib[..., 0::2] = words & 0xF
        nib[..., 1::2] = words >> 4
        vals = E2M1[nib]
    vals = vals * np.repeat(np.exp2(scales.astype(np.float64) - 127.0), 8, axis=1)[..., None]
    return vals.transpose(0, 1, 3, 2).reshape(g * 512, n)


B, S, D, H, HD = 1, 512, 8192, 8, 128
E = H * HD
EPS = 1e-5
NEG = -1e9


def get_slopes(n):
    start = 2.0 ** (-2.0 ** (-(np.log2(n) - 3)))
    return np.array([start * start ** i for i in range(n)])


def prior_bias(shape, scale, loc):
    q_pos = np.arange(S, dtype=np.float64)
    k_pos = np.arange(S, dtype=np.float64)
    dist = (k_pos[None, :] - q_pos[:, None])[None, None]
    loc_t = np.exp(loc) - np.exp(-loc)
    z = (dist - loc_t) * np.exp(scale)
    return -(np.abs(z) + EPS) ** shape


def setup_inputs():
    s = mx_kscale(D)
    causal = np.tril(np.ones((S, S), dtype=bool))
    x = bf(np.random.standard_normal((B, S, D)) * s)
    wv_words, wv_scales = pack_weight(np.random.standard_normal((D, E)) * 2.0 / np.sqrt(D) / s[:, None], "e4m3")
    return {"x": x,
            "wv_words": wv_words,
            "wv_scales": wv_scales,
            "q": bf(np.random.standard_normal((B, S, H, HD))),
            "k": bf(np.random.standard_normal((B, S, H, HD))),
            "mask": bf(np.where(causal, 0.0, NEG))[None, None],
            "shape": bf(1.0 + 0.1 * np.random.standard_normal((1, H, 1, 1))),
            "scale": bf(np.log(get_slopes(H)).reshape(1, H, 1, 1) + 0.1 * np.random.standard_normal((1, H, 1, 1))),
            "loc": bf(-2.0 + 0.5 * np.random.standard_normal((1, H, 1, 1)))}


def reference(x, wv_words, wv_scales, q, k, mask, shape, scale, loc):
    v = (mxq(f64(x), 2, "e4m3") @ unpack_weight(wv_words, wv_scales, "e4m3")).reshape(B, S, H, HD)
    s = f64(q).transpose(0, 2, 1, 3) @ f64(k).transpose(0, 2, 3, 1) / np.sqrt(HD)
    s = s + prior_bias(f64(shape), f64(scale), f64(loc))
    s = s + f64(mask)
    e = np.exp(s - s.max(-1, keepdims=True))
    o = (mxq(e, 3, "e4m3") @ mxq(v.transpose(0, 2, 1, 3), 2, "e4m3")) / e.sum(-1, keepdims=True)
    return o.transpose(0, 2, 1, 3).reshape(B, S, E)

@@ -1,0 +1,448 @@
+from contextlib import ExitStack
+import math
+
+import concourse.mybir as mybir
+from concourse.masks import make_identity
+
+BF16 = mybir.dt.bfloat16
+F32 = mybir.dt.float32
+I32 = mybir.dt.int32
+U32 = mybir.dt.uint32
+U8 = mybir.dt.uint8
+FP8X4 = mybir.dt.float8_e4m3fn_x4
+ACT = mybir.ActivationFunctionType
+ALU = mybir.AluOpType
+
+P = 128
+S = 512
+D = 8192
+H = 8
+HD = 128
+E = H * HD
+EPS = 1e-5
+
+S_TILES = S // P
+K_PASS = 4 * P
+PASSES = D // K_PASS
+CHUNK_PASSES = 2
+CHUNKS = PASSES // CHUNK_PASSES
+CHUNK_K = CHUNK_PASSES * K_PASS
+HALF = 512
+HALVES = E // HALF
+HALF_HEADS = HALF // HD
+PLANES = 4
+STREAM_BUFS = 4
+W_BUFS = 5
+
+PRIOR_W = 2 * S - P
+TABLE_ROWS = 32
+TABLE_HEADS = P // TABLE_ROWS
+TABLES = H // TABLE_HEADS
+TABLE_W = PRIOR_W + P - TABLE_ROWS
+SQUARINGS = 3
+EXP_HALVINGS = 10
+EXP_SERIES = (1.0, 1.0 / 2, 1.0 / 6, 1.0 / 24, 1.0 / 120)
+EXP_PLAIN = 3
+
+SCORE_TILES = H * S_TILES
+SCALAR_JOINS = 7
+FIRST_SCORE_PASS = 12
+TILES_A_PASS = 2
+
+FLOPS = 2 * S * D * E + 2 * 2 * H * S * S * HD
+
+
+def tile_bayesianattention_pa_k_kernel(
+    tc, x, wv_words, wv_scales, q, k, mask, shape, scale, loc, out
+):
+    nc = tc.nc
+
+    x_view = x.rearrange("b (u p r) k -> (b u) p r k", u=2, r=2)
+    w_view = wv_words.rearrange("g p n t -> g p (n t)").bitcast(I32).rearrange("g p n -> p g n")
+    w_scale_view = wv_scales.bitcast(I32)
+    q_view = q.rearrange("b (a p) h d -> p (b a) (h d)", p=P)
+    k_view = k.rearrange("b (a p) h d -> p (b a) (h d)", p=P)
+    mask_view = mask.rearrange("b c (a p) j -> p (b c a) j", p=P)
+    out_view = out.rearrange("b (a p) n -> p (b a) n", p=P)
+    scratch = out.rearrange("b s n -> (b s n)")[0 : H * TABLE_ROWS * TABLE_W].rearrange(
+        "(h r x) -> h r x", r=TABLE_ROWS, x=TABLE_W
+    )
+
+    with ExitStack() as ctx:
+        ctx.enter_context(tc.manual_schedule())
+        keep = ctx.enter_context(tc.tile_pool(name="keep", bufs=1))
+        stream = ctx.enter_context(tc.tile_pool(name="stream", bufs=STREAM_BUFS))
+        w_pool = ctx.enter_context(tc.tile_pool(name="w_pool", bufs=W_BUFS))
+        x_pool = ctx.enter_context(tc.tile_pool(name="x_pool", bufs=2))
+        v_psum = ctx.enter_context(tc.psum_pool(name="v_psum", bufs=1))
+        banks = ctx.enter_context(tc.psum_pool(name="banks", bufs=4))
+
+        ident_bf = keep.tile([P, P], BF16)
+        ident_f32 = keep.tile([P, P], F32)
+        prior = keep.tile([P, H, PRIOR_W], F32)
+        mask_sb = keep.tile([P, S_TILES, S], BF16)
+        qk_t = keep.tile([P, 2, H, S], BF16)
+        row_sum = keep.tile([P, S_TILES, H], F32)
+        w_planes = keep.tile([P, PASSES // PLANES, E], U8, align_bytes=64)
+        x_codes = keep.tile([P, PASSES, S], U32, align_bytes=64)
+        x_scales = keep.tile([P, PASSES, S], U8, align_bytes=64)
+        e_codes = keep.tile([P, H, S], U32, align_bytes=64)
+        e_scales = keep.tile([P, H, S], U8, align_bytes=64)
+        v_codes = keep.tile([P, HALVES, HALF], U32, align_bytes=64)
+        v_scales = keep.tile([P, HALVES, HALF], U8, align_bytes=64)
+        planes_words = w_planes[:].bitcast(I32)
+
+        x_tiles = {}
+        w_tiles = {}
+
+        def load_x(c):
+            x_sb = stream.tile([P, S_TILES, CHUNK_K], BF16, tag="stream", name="x_sb")
+            for u in range(2):
+                nc.sync.dma_start(
+                    out=x_sb[:, 2 * u : 2 * u + 2, :], in_=x_view[u][:, :, CHUNK_K * c : CHUNK_K * (c + 1)]
+                )
+            x_tiles[c] = x_sb
+
+        def load_w(i):
+            half, c = divmod(i, CHUNKS)
+            first_pass = CHUNK_PASSES * c
+            if half == 0 and first_pass % PLANES == 0:
+                for j in range(4):
+                    nc.sync.dma_start(
+                        out=planes_words[32 * j : 32 * j + 4 * PLANES, first_pass // PLANES, :],
+                        in_=w_scale_view[first_pass : first_pass + PLANES, 4 * j : 4 * j + 4, :],
+                    )
+            w_sb = w_pool.tile([P, CHUNK_PASSES, HALF], I32, align_bytes=64, name="w_sb")
+            nc.sync.dma_start(
+                out=w_sb[:], in_=w_view[:, first_pass : first_pass + CHUNK_PASSES, HALF * half : HALF * (half + 1)]
+            )
+            w_tiles[i] = w_sb
+
+        nc.vector.memset(w_planes[:].rearrange("p t n -> p (t n)").bitcast(I32), 0)
+        make_identity(nc, ident_bf[:])
+        make_identity(nc, ident_f32[:])
+
+        with tc.tile_pool(name="setup", bufs=1) as setup_pool:
+            scale_bf = setup_pool.tile([P, H], BF16)
+            loc_bf = setup_pool.tile([P, H], BF16)
+            shape_bf = setup_pool.tile([P, H], BF16)
+            nc.sync.dma_start(out=scale_bf[:], in_=scale.rearrange("a h b c -> (a h b c)").partition_broadcast(P))
+            nc.sync.dma_start(out=loc_bf[:], in_=loc.rearrange("a h b c -> (a h b c)").partition_broadcast(P))
+            nc.sync.dma_start(out=shape_bf[:], in_=shape.rearrange("a h b c -> (a h b c)").partition_broadcast(P))
+
+            q_sb = stream.tile([P, S_TILES, E], BF16, tag="stream")
+            k_sb = stream.tile([P, S_TILES, E], BF16, tag="stream")
+            nc.sync.dma_start(out=q_sb[:], in_=q_view)
+            nc.sync.dma_start(out=k_sb[:], in_=k_view)
+            load_x(0)
+            load_w(0)
+            nc.sync.dma_start(out=mask_sb[:], in_=mask_view)
+            load_x(1)
+            load_w(1)
+
+            for which, rows_sb in ((0, q_sb), (1, k_sb)):
+                for pair in range(H // 2):
+                    qk_ps = banks.tile([P, 2, S], BF16, tag="bank")
+                    for i in range(2):
+                        head = slice(HD * (2 * pair + i), HD * (2 * pair + i + 1))
+                        for a in range(S_TILES):
+                            nc.tensor.transpose(qk_ps[:, i, P * a : P * (a + 1)], rows_sb[:, a, head], ident_bf[:])
+                    nc.scalar.copy(out=qk_t[:, which, 2 * pair : 2 * pair + 2, :], in_=qk_ps[:])
+            load_x(2)
+            load_w(2)
+            load_x(3)
+            load_w(3)
+            load_w(4)
+
+
+            exponent = setup_pool.tile([P, 3, TABLES], F32)
+            shape_col = setup_pool.tile([P, TABLES], F32)
+            shift_col = setup_pool.tile([P, 1], F32)
+            eps_col = setup_pool.tile([P, 1], F32)
+            nc.vector.memset(eps_col[:], EPS)
+            for i in range(TABLE_HEADS):
+                rows = slice(TABLE_ROWS * i, TABLE_ROWS * (i + 1))
+                nc.vector.memset(shift_col[rows, :], float(TABLE_ROWS * i - (S - TABLE_ROWS)))
+                nc.vector.tensor_copy(out=exponent[rows, 0, :], in_=scale_bf[rows, i::TABLE_HEADS])
+                nc.vector.tensor_copy(out=exponent[rows, 1, :], in_=loc_bf[rows, i::TABLE_HEADS])
+                nc.vector.tensor_copy(out=shape_col[rows, :], in_=shape_bf[rows, i::TABLE_HEADS])
+            nc.vector.tensor_scalar_mul(out=exponent[:, 2, :], in0=exponent[:, 1, :], scalar1=-1.0)
+
+            small = setup_pool.tile([P, 3, TABLES], F32)
+            grown = setup_pool.tile([P, 3, TABLES], F32)
+            nc.vector.tensor_scalar_mul(out=small[:], in0=exponent[:], scalar1=1.0 / 2**EXP_HALVINGS)
+            nc.vector.tensor_scalar_mul(out=grown[:], in0=small[:], scalar1=EXP_SERIES[-1])
+            for coefficient in reversed(EXP_SERIES[:-1]):
+                nc.vector.scalar_tensor_tensor(
+                    out=grown[:], in0=grown[:], scalar=coefficient, in1=small[:], op0=ALU.add, op1=ALU.mult
+                )
+            for squaring in range(EXP_HALVINGS - EXP_PLAIN):
+                nc.vector.scalar_tensor_tensor(
+                    out=grown[:], in0=grown[:], scalar=2.0, in1=grown[:], op0=ALU.add, op1=ALU.mult
+                )
+            nc.vector.tensor_scalar_add(out=grown[:], in0=grown[:], scalar1=1.0)
+            for squaring in range(EXP_PLAIN):
+                nc.vector.tensor_mul(out=grown[:], in0=grown[:], in1=grown[:])
+            slope_col = grown[:, 0, :]
+            neg_offset = setup_pool.tile([P, TABLES], F32)
+            nc.vector.tensor_sub(out=neg_offset[:], in0=grown[:, 2, :], in1=grown[:, 1, :])
+            root_col = setup_pool.tile([P, TABLES], F32)
+            nc.vector.tensor_scalar(
+                out=root_col[:],
+                in0=shape_col[:],
+                scalar1=1.0,
+                scalar2=1.0 / 2**SQUARINGS,
+                op0=ALU.subtract,
+                op1=ALU.mult,
+            )
+
+            count_i = setup_pool.tile([P, TABLE_W], I32)
+            dist = setup_pool.tile([P, TABLE_W], F32)
+            nc.gpsimd.iota(count_i[:], pattern=[[1, TABLE_W]], base=0, channel_multiplier=-1)
+            nc.vector.tensor_scalar(
+                out=dist[:], in0=count_i[:], scalar1=shift_col[:, 0:1], scalar2=None, op0=ALU.add
+            )
+
+            work = [setup_pool.tile([P, TABLE_W], F32, name="work%d" % t) for t in range(TABLES)]
+            base = [setup_pool.tile([P, TABLE_W], F32, name="base%d" % t) for t in range(TABLES)]
+            for t in range(TABLES):
+                nc.scalar.activation(out=work[t][:], in_=dist[:], func=ACT.Abs, bias=neg_offset[:, t : t + 1])
+                nc.gpsimd.tensor_scalar(
+                    out=base[t][:],
+                    in0=work[t][:],
+                    scalar1=slope_col[:, t : t + 1],
+                    scalar2=EPS,
+                    op0=ALU.mult,
+                    op1=ALU.add,
+                )
+            for t in range(TABLES):
+                nc.scalar.activation(
+                    out=work[t][:], in_=work[t][:], func=ACT.Ln, scale=slope_col[:, t : t + 1], bias=eps_col[:, 0:1]
+                )
+            for t in range(TABLES):
+                nc.scalar.activation(out=work[t][:], in_=work[t][:], func=ACT.Exp, scale=root_col[:, t : t + 1])
+                for squaring in range(SQUARINGS):
+                    nc.scalar.activation(out=work[t][:], in_=work[t][:], func=ACT.Square)
+                nc.gpsimd.tensor_tensor(out=base[t][:], in0=base[t][:], in1=work[t][:], op=ALU.mult)
+                heads = slice(TABLE_HEADS * t, TABLE_HEADS * (t + 1))
+                nc.gpsimd.dma_start(out=scratch[heads].rearrange("h r x -> (h r) x"), in_=base[t][:])
+            for t in range(TABLES):
+                heads = slice(TABLE_HEADS * t, TABLE_HEADS * (t + 1))
+                for j in range(P // TABLE_ROWS):
+                    first = P - TABLE_ROWS - TABLE_ROWS * j
+                    nc.gpsimd.dma_start(
+                        out=prior[TABLE_ROWS * j : TABLE_ROWS * (j + 1), heads, :],
+                        in_=scratch[heads].rearrange("h r x -> r h x")[:, :, first : first + PRIOR_W],
+                    )
+
+        score_pool = ctx.enter_context(tc.tile_pool(name="score_pool", bufs=4, reuse_waits="tile"))
+        e_pool = ctx.enter_context(tc.tile_pool(name="e_pool", bufs=2, reuse_waits="tile"))
+        v_pool = ctx.enter_context(tc.tile_pool(name="v_pool", bufs=1, reuse_waits="tile"))
+        o_pool = ctx.enter_context(tc.tile_pool(name="o_pool", bufs=3, reuse_waits="tile"))
+
+        x_grouped = {}
+        added = {}
+        e_heads = {}
+        e_grouped = {}
+
+        def add_mask(h):
+            added[h] = stream.tile([P, S_TILES, S], F32, tag="stream", name="added")
+            for a in range(S_TILES):
+                first = S - P - P * a
+                nc.gpsimd.tensor_tensor(
+                    out=added[h][:, a, :], in0=prior[:, h, first : first + S], in1=mask_sb[:, a, :], op=ALU.subtract
+                )
+
+        def transpose_x(g):
+            c, local = divmod(g, CHUNK_PASSES)
+            x_words = x_tiles[c][:].bitcast(F32)
+            grouped = x_pool.tile([P, 4 * S], BF16, align_bytes=64, name="x_grouped")
+            grouped_words = grouped[:].bitcast(F32).rearrange("p (s w) -> p s w", w=2)
+            first = (K_PASS // 2) * local
+            for b in range(S_TILES // 2):
+                xt_ps = banks.tile([P, 2, 2 * P], F32, tag="bank")
+                for m in range(2):
+                    for w in range(2):
+                        nc.tensor.transpose(
+                            xt_ps[:, w, P * m : P * (m + 1)],
+                            x_words[:, 2 * b + m, first + w : first + K_PASS // 2 : 2],
+                            ident_f32[:],
+                        )
+                side_by_side = grouped_words[:, 2 * P * b : 2 * P * (b + 1), :]
+                if b == 1 and g >= SCALAR_JOINS:
+                    nc.scalar.copy(out=side_by_side, in_=xt_ps[:].rearrange("p w s -> p s w"))
+                else:
+                    nc.vector.tensor_copy(out=side_by_side, in_=xt_ps[:].rearrange("p w s -> p s w"))
+            x_grouped[g] = grouped
+            if local == CHUNK_PASSES - 1:
+                if c + STREAM_BUFS < CHUNKS:
+                    load_x(c + STREAM_BUFS)
+                else:
+                    add_mask(c + STREAM_BUFS - CHUNKS)
+
+        def quantise_x(g):
+            nc.vector.quantize_mx(
+                out=x_codes[:, g, :].bitcast(FP8X4), scales=x_scales[:, g, :], in_=x_grouped[g][:]
+            )
+
+        def project(v_ps, half, g):
+            c, local = divmod(g, CHUNK_PASSES)
+            i = CHUNKS * half + c
+            plane = PLANES * (g % PLANES)
+            for m in range(S_TILES):
+                cols = slice(P * m, P * (m + 1))
+                nc.tensor.matmul_mx(
+                    out=v_ps[m][:],
+                    lhsT=x_codes[:, g, cols].bitcast(FP8X4),
+                    lhsT_scale=x_scales[:, g, cols],
+                    rhs=w_tiles[i][:, local, :].bitcast(FP8X4),
+                    rhs_scale=w_planes[plane:P, g // PLANES, HALF * half : HALF * (half + 1)],
+                    start=(g == 0),
+                    stop=(g == PASSES - 1),
+                )
+            if local == CHUNK_PASSES - 1 and i + W_BUFS < HALVES * CHUNKS:
+                load_w(i + W_BUFS)
+
+        def score_tiles(first_tile, count):
+            tiles = [divmod(n, S_TILES) for n in range(first_tile, first_tile + count)]
+            s_ps = {}
+            neg_s = {}
+            neg_max = {}
+            for h, a in tiles:
+                if a == 0:
+                    e_heads[h] = e_pool.tile([P, S_TILES, S], BF16, name="e_head")
+                s_ps[a] = banks.tile([P, S], F32, tag="bank", name="s_ps")
+                nc.tensor.matmul(
+                    s_ps[a][:], lhsT=qk_t[:, 0, h, P * a : P * (a + 1)], rhs=qk_t[:, 1, h, :], start=True, stop=True
+                )
+            for h, a in tiles:
+                neg_s[a] = score_pool.tile([P, S], F32, name="neg_s")
+                nc.vector.scalar_tensor_tensor(
+                    out=neg_s[a][:],
+                    in0=s_ps[a][:],
+                    scalar=-1.0 / math.sqrt(HD),
+                    in1=added[h][:, a, :],
+                    op0=ALU.mult,
+                    op1=ALU.add,
+                )
+                if a == S_TILES - 1 and h + STREAM_BUFS < H:
+                    add_mask(h + STREAM_BUFS)
+            for h, a in tiles:
+                neg_max[a] = score_pool.tile([P, 1], F32, name="neg_max")
+                nc.vector.tensor_scalar(
+                    out=neg_s[a][:],
+                    in0=neg_s[a][:],
+                    scalar1=1.0,
+                    scalar2=None,
+                    op0=ALU.mult,
+                    op1=ALU.min,
+                    accum_out=neg_max[a][:],
+                )
+            for h, a in tiles:
+                nc.scalar.activation(
+                    out=e_heads[h][:, a, :],
+                    in_=neg_s[a][:],
+                    func=ACT.Exp,
+                    scale=-1.0,
+                    bias=neg_max[a][:, 0:1],
+                    accum_out=row_sum[:, a, h : h + 1],
+                )
+
+        def transpose_e(h):
+            grouped = e_pool.tile([P, 4 * S], BF16, align_bytes=64, name="e_grouped")
+            grouped_words = grouped[:].bitcast(F32).rearrange("p (i u) -> p i u", u=2)
+            for b in range(S_TILES // 2):
+                et_ps = banks.tile([P, 2, 2 * P], F32, tag="bank")
+                for m in range(2):
+                    e_words = e_heads[h][:, 2 * b + m, :].bitcast(F32)
+                    for u in range(2):
+                        nc.tensor.transpose(
+                            et_ps[:, u, P * m : P * (m + 1)], e_words[:, P * u : P * (u + 1)], ident_f32[:]
+                        )
+                nc.scalar.copy(
+                    out=grouped_words[:, 2 * P * b : 2 * P * (b + 1), :], in_=et_ps[:].rearrange("p u i -> p i u")
+                )
+            e_grouped[h] = grouped
+
+        def quantise_e(h):
+            nc.vector.quantize_mx(out=e_codes[:, h, :].bitcast(FP8X4), scales=e_scales[:, h, :], in_=e_grouped[h][:])
+
+        def quantise_v(v_ps, half):
+            v_bf = v_pool.tile([P, S_TILES, HALF], BF16)
+            for m in range(S_TILES):
+                if m % 2 == 0:
+                    nc.scalar.copy(out=v_bf[:, m, :], in_=v_ps[m][:])
+                else:
+                    nc.vector.tensor_copy(out=v_bf[:, m, :], in_=v_ps[m][:])
+            grouped = v_pool.tile([P, HALF, S_TILES], BF16, align_bytes=64, name="v_grouped")
+            nc.vector.tensor_copy(out=grouped[:], in_=v_bf[:].rearrange("p m n -> p n m"))
+            nc.vector.quantize_mx(
+                out=v_codes[:, half, :].bitcast(FP8X4),
+                scales=v_scales[:, half, :],
+                in_=grouped[:].rearrange("p n m -> p (n m)"),
+            )
+
+        def invert_sums(half):
+            inv_sum = o_pool.tile([P, S_TILES, HALF_HEADS], F32)
+            nc.vector.reciprocal(out=inv_sum[:], in_=row_sum[:, :, HALF_HEADS * half : HALF_HEADS * (half + 1)])
+            return inv_sum
+
+        def attend(inv_sum, half, a):
+            rows = slice(P * a, P * (a + 1))
+            o_ps = banks.tile([P, HALF_HEADS, HD], F32, tag="bank")
+            for i in range(HALF_HEADS):
+                h = HALF_HEADS * half + i
+                cols = slice(HD * i, HD * (i + 1))
+                nc.tensor.matmul_mx(
+                    out=o_ps[:, i, :],
+                    lhsT=e_codes[:, h, rows].bitcast(FP8X4),
+                    lhsT_scale=e_scales[:, h, rows],
+                    rhs=v_codes[:, half, cols].bitcast(FP8X4),
+                    rhs_scale=v_scales[:, half, cols],
+                    start=True,
+                    stop=True,
+                )
+            o_sb = o_pool.tile([P, HALF_HEADS, HD], F32)
+            nc.vector.tensor_tensor(
+                out=o_sb[:],
+                in0=o_ps[:],
+                in1=inv_sum[:, a, :].unsqueeze(2).to_broadcast([P, HALF_HEADS, HD]),
+                op=ALU.mult,
+            )
+            nc.sync.dma_start(
+                out=out_view[:, a, HALF * half : HALF * (half + 1)], in_=o_sb[:].rearrange("p h d -> p (h d)")
+            )
+
+        v_ps = [v_psum.tile([P, HALF], F32, name="v_ps%d" % m, tag="v_ps%d" % m) for m in range(S_TILES)]
+        for g in range(PASSES + 1):
+            if g > 0:
+                quantise_x(g - 1)
+            if g < PASSES:
+                transpose_x(g)
+            if g > 0:
+                project(v_ps, 0, g - 1)
+            if FIRST_SCORE_PASS <= g < PASSES:
+                score_tiles(g - FIRST_SCORE_PASS, 1)
+        quantise_v(v_ps, 0)
+
+        done_before = PASSES - FIRST_SCORE_PASS
+        first_attend = 2 * HALF_HEADS + 1
+        v_ps = [v_psum.tile([P, HALF], F32, name="v_ps%d" % m, tag="v_ps%d" % m) for m in range(S_TILES)]
+        for g in range(PASSES):
+            project(v_ps, 1, g)
+            if g == first_attend:
+                inv_sum = invert_sums(0)
+            if first_attend <= g < first_attend + S_TILES:
+                attend(inv_sum, 0, g - first_attend)
+            if g % 2 == 1:
+                transpose_e(g // 2)
+            elif g > 0:
+                quantise_e(g // 2 - 1)
+            first_tile = done_before + TILES_A_PASS * g
+            if first_tile < SCORE_TILES:
+                score_tiles(first_tile, TILES_A_PASS)
+        quantise_e(H - 1)
+        quantise_v(v_ps, 1)
+        inv_sum = invert_sums(1)
+        for a in range(S_TILES):
+            attend(inv_sum, 1, a)

@@ -34,7 +34,7 @@ PLANES = 4
 STREAM_BUFS = 4
 W_BUFS = 5
 
-PRIOR_W = 2 * S - P
+PRIOR_W = S
 TABLE_ROWS = 32
 TABLE_HEADS = P // TABLE_ROWS
 TABLES = H // TABLE_HEADS
@@ -45,9 +45,10 @@ EXP_SERIES = (1.0, 1.0 / 2, 1.0 / 6, 1.0 / 24, 1.0 / 120)
 EXP_PLAIN = 3
 
 SCORE_TILES = H * S_TILES
-SCALAR_JOINS = 7
-FIRST_SCORE_PASS = 12
+SCALAR_JOINS = 5
+SPREAD_PASS = 5
 TILES_A_PASS = 2
+FIRST_SCORE_PASS = PASSES - S_TILES // TILES_A_PASS
 
 FLOPS = 2 * S * D * E + 2 * 2 * H * S * S * HD
 
@@ -80,7 +81,10 @@ def tile_bayesianattention_pa_k_kernel(
         ident_bf = keep.tile([P, P], BF16)
         ident_f32 = keep.tile([P, P], F32)
         prior = keep.tile([P, H, PRIOR_W], F32)
-        mask_sb = keep.tile([P, S_TILES, S], BF16)
+        mask_diag = keep.tile([P, S_TILES, P], BF16)
+        diag = keep.tile([P, H, S_TILES, P], F32)
+        e_heads = [keep.tile([P, S_TILES, S], BF16, name="e_head%d" % i) for i in range(2)]
+        e_grouped = [keep.tile([P, 4 * S], BF16, align_bytes=64, name="e_grouped%d" % i) for i in range(2)]
         qk_t = keep.tile([P, 2, H, S], BF16)
         row_sum = keep.tile([P, S_TILES, H], F32)
         w_planes = keep.tile([P, PASSES // PLANES, E], U8, align_bytes=64)
@@ -91,6 +95,7 @@ def tile_bayesianattention_pa_k_kernel(
         v_codes = keep.tile([P, HALVES, HALF], U32, align_bytes=64)
         v_scales = keep.tile([P, HALVES, HALF], U8, align_bytes=64)
         planes_words = w_planes[:].bitcast(I32)
+        base = [keep.tile([P, TABLE_W], F32, name="base%d" % t) for t in range(TABLES)]
 
         x_tiles = {}
         w_tiles = {}
@@ -119,6 +124,9 @@ def tile_bayesianattention_pa_k_kernel(
             w_tiles[i] = w_sb
 
         nc.vector.memset(w_planes[:].rearrange("p t n -> p (t n)").bitcast(I32), 0)
+        for i in range(2):
+            nc.vector.memset(e_heads[i][:].rearrange("p a j -> p (a j)").bitcast(I32), 0)
+            nc.vector.memset(e_grouped[i][:].bitcast(I32), 0)
         make_identity(nc, ident_bf[:])
         make_identity(nc, ident_f32[:])
 
@@ -136,9 +144,10 @@ def tile_bayesianattention_pa_k_kernel(
             nc.sync.dma_start(out=k_sb[:], in_=k_view)
             load_x(0)
             load_w(0)
-            nc.sync.dma_start(out=mask_sb[:], in_=mask_view)
             load_x(1)
             load_w(1)
+            for a in range(S_TILES):
+                nc.sync.dma_start(out=mask_diag[:, a, :], in_=mask_view[:, a, P * a : P * (a + 1)])
 
             for which, rows_sb in ((0, q_sb), (1, k_sb)):
                 for pair in range(H // 2):
@@ -204,7 +213,6 @@ def tile_bayesianattention_pa_k_kernel(
             )
 
             work = [setup_pool.tile([P, TABLE_W], F32, name="work%d" % t) for t in range(TABLES)]
-            base = [setup_pool.tile([P, TABLE_W], F32, name="base%d" % t) for t in range(TABLES)]
             for t in range(TABLES):
                 nc.scalar.activation(out=work[t][:], in_=dist[:], func=ACT.Abs, bias=neg_offset[:, t : t + 1])
                 nc.gpsimd.tensor_scalar(
@@ -224,33 +232,31 @@ def tile_bayesianattention_pa_k_kernel(
                 for squaring in range(SQUARINGS):
                     nc.scalar.activation(out=work[t][:], in_=work[t][:], func=ACT.Square)
                 nc.gpsimd.tensor_tensor(out=base[t][:], in0=base[t][:], in1=work[t][:], op=ALU.mult)
-                heads = slice(TABLE_HEADS * t, TABLE_HEADS * (t + 1))
-                nc.gpsimd.dma_start(out=scratch[heads].rearrange("h r x -> (h r) x"), in_=base[t][:])
-            for t in range(TABLES):
-                heads = slice(TABLE_HEADS * t, TABLE_HEADS * (t + 1))
-                for j in range(P // TABLE_ROWS):
-                    first = P - TABLE_ROWS - TABLE_ROWS * j
-                    nc.gpsimd.dma_start(
-                        out=prior[TABLE_ROWS * j : TABLE_ROWS * (j + 1), heads, :],
-                        in_=scratch[heads].rearrange("h r x -> r h x")[:, :, first : first + PRIOR_W],
-                    )
 
         score_pool = ctx.enter_context(tc.tile_pool(name="score_pool", bufs=4, reuse_waits="tile"))
-        e_pool = ctx.enter_context(tc.tile_pool(name="e_pool", bufs=2, reuse_waits="tile"))
         v_pool = ctx.enter_context(tc.tile_pool(name="v_pool", bufs=1, reuse_waits="tile"))
         o_pool = ctx.enter_context(tc.tile_pool(name="o_pool", bufs=3, reuse_waits="tile"))
 
         x_grouped = {}
-        added = {}
-        e_heads = {}
-        e_grouped = {}
 
-        def add_mask(h):
-            added[h] = stream.tile([P, S_TILES, S], F32, tag="stream", name="added")
-            for a in range(S_TILES):
-                first = S - P - P * a
+        def spread_prior():
+            for t in range(TABLES):
+                heads = slice(TABLE_HEADS * t, TABLE_HEADS * (t + 1))
+                nc.sync.dma_start(out=scratch[heads].rearrange("h r x -> (h r) x"), in_=base[t][:])
+            for t in range(TABLES):
+                heads = slice(TABLE_HEADS * t, TABLE_HEADS * (t + 1))
+                for j in range(P // TABLE_ROWS):
+                    first = P - TABLE_ROWS - TABLE_ROWS * j
+                    nc.sync.dma_start(
+                        out=prior[TABLE_ROWS * j : TABLE_ROWS * (j + 1), heads, :],
+                        in_=scratch[heads].rearrange("h r x -> r h x")[:, :, first : first + PRIOR_W],
+                    )
+            for h in range(H):
                 nc.gpsimd.tensor_tensor(
-                    out=added[h][:, a, :], in0=prior[:, h, first : first + S], in1=mask_sb[:, a, :], op=ALU.subtract
+                    out=diag[:, h],
+                    in0=prior[:, h, S - P : S].unsqueeze(1).to_broadcast([P, S_TILES, P]),
+                    in1=mask_diag[:],
+                    op=ALU.subtract,
                 )
 
         def transpose_x(g):
@@ -274,11 +280,8 @@ def tile_bayesianattention_pa_k_kernel(
                 else:
                     nc.vector.tensor_copy(out=side_by_side, in_=xt_ps[:].rearrange("p w s -> p s w"))
             x_grouped[g] = grouped
-            if local == CHUNK_PASSES - 1:
-                if c + STREAM_BUFS < CHUNKS:
-                    load_x(c + STREAM_BUFS)
-                else:
-                    add_mask(c + STREAM_BUFS - CHUNKS)
+            if local == CHUNK_PASSES - 1 and c + STREAM_BUFS < CHUNKS:
+                load_x(c + STREAM_BUFS)
 
         def quantise_x(g):
             nc.vector.quantize_mx(
@@ -309,29 +312,39 @@ def tile_bayesianattention_pa_k_kernel(
             neg_s = {}
             neg_max = {}
             for h, a in tiles:
-                if a == 0:
-                    e_heads[h] = e_pool.tile([P, S_TILES, S], BF16, name="e_head")
                 s_ps[a] = banks.tile([P, S], F32, tag="bank", name="s_ps")
                 nc.tensor.matmul(
-                    s_ps[a][:], lhsT=qk_t[:, 0, h, P * a : P * (a + 1)], rhs=qk_t[:, 1, h, :], start=True, stop=True
+                    s_ps[a][:, 0 : P * (a + 1)],
+                    lhsT=qk_t[:, 0, h, P * a : P * (a + 1)],
+                    rhs=qk_t[:, 1, h, 0 : P * (a + 1)],
+                    start=True,
+                    stop=True,
                 )
             for h, a in tiles:
                 neg_s[a] = score_pool.tile([P, S], F32, name="neg_s")
+                own = slice(P * a, P * (a + 1))
                 nc.vector.scalar_tensor_tensor(
-                    out=neg_s[a][:],
-                    in0=s_ps[a][:],
+                    out=neg_s[a][:, own],
+                    in0=s_ps[a][:, own],
                     scalar=-1.0 / math.sqrt(HD),
-                    in1=added[h][:, a, :],
+                    in1=diag[:, h, a, :],
                     op0=ALU.mult,
                     op1=ALU.add,
                 )
-                if a == S_TILES - 1 and h + STREAM_BUFS < H:
-                    add_mask(h + STREAM_BUFS)
+                if a > 0:
+                    nc.vector.scalar_tensor_tensor(
+                        out=neg_s[a][:, 0 : P * a],
+                        in0=s_ps[a][:, 0 : P * a],
+                        scalar=-1.0 / math.sqrt(HD),
+                        in1=prior[:, h, S - P - P * a : S - P],
+                        op0=ALU.mult,
+                        op1=ALU.add,
+                    )
             for h, a in tiles:
                 neg_max[a] = score_pool.tile([P, 1], F32, name="neg_max")
                 nc.vector.tensor_scalar(
-                    out=neg_s[a][:],
-                    in0=neg_s[a][:],
+                    out=neg_s[a][:, 0 : P * (a + 1)],
+                    in0=neg_s[a][:, 0 : P * (a + 1)],
                     scalar1=1.0,
                     scalar2=None,
                     op0=ALU.mult,
@@ -340,8 +353,8 @@ def tile_bayesianattention_pa_k_kernel(
                 )
             for h, a in tiles:
                 nc.scalar.activation(
-                    out=e_heads[h][:, a, :],
-                    in_=neg_s[a][:],
+                    out=e_heads[h % 2][:, a, 0 : P * (a + 1)],
+                    in_=neg_s[a][:, 0 : P * (a + 1)],
                     func=ACT.Exp,
                     scale=-1.0,
                     bias=neg_max[a][:, 0:1],
@@ -349,23 +362,24 @@ def tile_bayesianattention_pa_k_kernel(
                 )
 
         def transpose_e(h):
-            grouped = e_pool.tile([P, 4 * S], BF16, align_bytes=64, name="e_grouped")
-            grouped_words = grouped[:].bitcast(F32).rearrange("p (i u) -> p i u", u=2)
-            for b in range(S_TILES // 2):
-                et_ps = banks.tile([P, 2, 2 * P], F32, tag="bank")
-                for m in range(2):
-                    e_words = e_heads[h][:, 2 * b + m, :].bitcast(F32)
-                    for u in range(2):
-                        nc.tensor.transpose(
-                            et_ps[:, u, P * m : P * (m + 1)], e_words[:, P * u : P * (u + 1)], ident_f32[:]
-                        )
-                nc.scalar.copy(
-                    out=grouped_words[:, 2 * P * b : 2 * P * (b + 1), :], in_=et_ps[:].rearrange("p u i -> p i u")
-                )
-            e_grouped[h] = grouped
+            e_words = e_heads[h % 2][:].bitcast(F32)
+            grouped_words = e_grouped[h % 2][:].bitcast(F32).rearrange("p (i u) -> p i u", u=2)
+            low_ps = banks.tile([P, 2 * P], F32, tag="bank")
+            for a in range(2):
+                nc.tensor.transpose(low_ps[:, P * a : P * (a + 1)], e_words[:, a, 0:P], ident_f32[:])
+            nc.scalar.copy(out=grouped_words[:, 0 : 2 * P, 0], in_=low_ps[:])
+            high_ps = banks.tile([P, 2, 2 * P], F32, tag="bank")
+            for a in range(2, S_TILES):
+                for u in range(2):
+                    nc.tensor.transpose(
+                        high_ps[:, u, P * (a - 2) : P * (a - 1)], e_words[:, a, P * u : P * (u + 1)], ident_f32[:]
+                    )
+            nc.scalar.copy(out=grouped_words[:, 2 * P : 4 * P, :], in_=high_ps[:].rearrange("p u i -> p i u"))
 
         def quantise_e(h):
-            nc.vector.quantize_mx(out=e_codes[:, h, :].bitcast(FP8X4), scales=e_scales[:, h, :], in_=e_grouped[h][:])
+            nc.vector.quantize_mx(
+                out=e_codes[:, h, :].bitcast(FP8X4), scales=e_scales[:, h, :], in_=e_grouped[h % 2][:]
+            )
 
         def quantise_v(v_ps, half):
             v_bf = v_pool.tile([P, S_TILES, HALF], BF16)
@@ -421,11 +435,13 @@ def tile_bayesianattention_pa_k_kernel(
                 transpose_x(g)
             if g > 0:
                 project(v_ps, 0, g - 1)
+            if g == SPREAD_PASS:
+                spread_prior()
             if FIRST_SCORE_PASS <= g < PASSES:
-                score_tiles(g - FIRST_SCORE_PASS, 1)
+                score_tiles(TILES_A_PASS * (g - FIRST_SCORE_PASS), TILES_A_PASS)
         quantise_v(v_ps, 0)
 
-        done_before = PASSES - FIRST_SCORE_PASS
+        done_before = TILES_A_PASS * (PASSES - FIRST_SCORE_PASS)
         first_attend = 2 * HALF_HEADS + 1
         v_ps = [v_psum.tile([P, HALF], F32, name="v_ps%d" % m, tag="v_ps%d" % m) for m in range(S_TILES)]
         for g in range(PASSES):

@@ -35,20 +35,16 @@ STREAM_BUFS = 4
 W_BUFS = 5
 
 PRIOR_W = S
-TABLE_ROWS = 32
-TABLE_HEADS = P // TABLE_ROWS
-TABLES = H // TABLE_HEADS
-TABLE_W = PRIOR_W + P - TABLE_ROWS
 SQUARINGS = 3
 EXP_HALVINGS = 10
 EXP_SERIES = (1.0, 1.0 / 2, 1.0 / 6, 1.0 / 24, 1.0 / 120)
 EXP_PLAIN = 3
 
 SCORE_TILES = H * S_TILES
-SCALAR_JOINS = 5
-SPREAD_PASS = 5
-TILES_A_PASS = 2
-FIRST_SCORE_PASS = PASSES - S_TILES // TILES_A_PASS
+SLOTS = HALVES * PASSES
+FIRST_SCORE_SLOT = 12
+TILES_A_SLOT = 2
+HEAD_SLOTS = S_TILES // TILES_A_SLOT
 
 FLOPS = 2 * S * D * E + 2 * 2 * H * S * S * HD
 
@@ -65,9 +61,6 @@ def tile_bayesianattention_pa_k_kernel(
     k_view = k.rearrange("b (a p) h d -> p (b a) (h d)", p=P)
     mask_view = mask.rearrange("b c (a p) j -> p (b c a) j", p=P)
     out_view = out.rearrange("b (a p) n -> p (b a) n", p=P)
-    scratch = out.rearrange("b s n -> (b s n)")[0 : H * TABLE_ROWS * TABLE_W].rearrange(
-        "(h r x) -> h r x", r=TABLE_ROWS, x=TABLE_W
-    )
 
     with ExitStack() as ctx:
         ctx.enter_context(tc.manual_schedule())
@@ -95,7 +88,6 @@ def tile_bayesianattention_pa_k_kernel(
         v_codes = keep.tile([P, HALVES, HALF], U32, align_bytes=64)
         v_scales = keep.tile([P, HALVES, HALF], U8, align_bytes=64)
         planes_words = w_planes[:].bitcast(I32)
-        base = [keep.tile([P, TABLE_W], F32, name="base%d" % t) for t in range(TABLES)]
 
         x_tiles = {}
         w_tiles = {}
@@ -149,36 +141,16 @@ def tile_bayesianattention_pa_k_kernel(
             for a in range(S_TILES):
                 nc.sync.dma_start(out=mask_diag[:, a, :], in_=mask_view[:, a, P * a : P * (a + 1)])
 
-            for which, rows_sb in ((0, q_sb), (1, k_sb)):
-                for pair in range(H // 2):
-                    qk_ps = banks.tile([P, 2, S], BF16, tag="bank")
-                    for i in range(2):
-                        head = slice(HD * (2 * pair + i), HD * (2 * pair + i + 1))
-                        for a in range(S_TILES):
-                            nc.tensor.transpose(qk_ps[:, i, P * a : P * (a + 1)], rows_sb[:, a, head], ident_bf[:])
-                    nc.scalar.copy(out=qk_t[:, which, 2 * pair : 2 * pair + 2, :], in_=qk_ps[:])
-            load_x(2)
-            load_w(2)
-            load_x(3)
-            load_w(3)
-            load_w(4)
 
-
-            exponent = setup_pool.tile([P, 3, TABLES], F32)
-            shape_col = setup_pool.tile([P, TABLES], F32)
-            shift_col = setup_pool.tile([P, 1], F32)
+            exponent = setup_pool.tile([P, 3, H], F32)
             eps_col = setup_pool.tile([P, 1], F32)
             nc.vector.memset(eps_col[:], EPS)
-            for i in range(TABLE_HEADS):
-                rows = slice(TABLE_ROWS * i, TABLE_ROWS * (i + 1))
-                nc.vector.memset(shift_col[rows, :], float(TABLE_ROWS * i - (S - TABLE_ROWS)))
-                nc.vector.tensor_copy(out=exponent[rows, 0, :], in_=scale_bf[rows, i::TABLE_HEADS])
-                nc.vector.tensor_copy(out=exponent[rows, 1, :], in_=loc_bf[rows, i::TABLE_HEADS])
-                nc.vector.tensor_copy(out=shape_col[rows, :], in_=shape_bf[rows, i::TABLE_HEADS])
-            nc.vector.tensor_scalar_mul(out=exponent[:, 2, :], in0=exponent[:, 1, :], scalar1=-1.0)
+            nc.vector.tensor_copy(out=exponent[:, 0, :], in_=scale_bf[:])
+            nc.vector.tensor_copy(out=exponent[:, 1, :], in_=loc_bf[:])
+            nc.vector.tensor_scalar_mul(out=exponent[:, 2, :], in0=loc_bf[:], scalar1=-1.0)
 
-            small = setup_pool.tile([P, 3, TABLES], F32)
-            grown = setup_pool.tile([P, 3, TABLES], F32)
+            small = setup_pool.tile([P, 3, H], F32)
+            grown = setup_pool.tile([P, 3, H], F32)
             nc.vector.tensor_scalar_mul(out=small[:], in0=exponent[:], scalar1=1.0 / 2**EXP_HALVINGS)
             nc.vector.tensor_scalar_mul(out=grown[:], in0=small[:], scalar1=EXP_SERIES[-1])
             for coefficient in reversed(EXP_SERIES[:-1]):
@@ -192,72 +164,79 @@ def tile_bayesianattention_pa_k_kernel(
             nc.vector.tensor_scalar_add(out=grown[:], in0=grown[:], scalar1=1.0)
             for squaring in range(EXP_PLAIN):
                 nc.vector.tensor_mul(out=grown[:], in0=grown[:], in1=grown[:])
-            slope_col = grown[:, 0, :]
-            neg_offset = setup_pool.tile([P, TABLES], F32)
+            slope = grown[:, 0, :]
+            neg_offset = setup_pool.tile([P, H], F32)
             nc.vector.tensor_sub(out=neg_offset[:], in0=grown[:, 2, :], in1=grown[:, 1, :])
-            root_col = setup_pool.tile([P, TABLES], F32)
+            root = setup_pool.tile([P, H], F32)
             nc.vector.tensor_scalar(
-                out=root_col[:],
-                in0=shape_col[:],
+                out=root[:],
+                in0=shape_bf[:],
                 scalar1=1.0,
                 scalar2=1.0 / 2**SQUARINGS,
                 op0=ALU.subtract,
                 op1=ALU.mult,
             )
 
-            count_i = setup_pool.tile([P, TABLE_W], I32)
-            dist = setup_pool.tile([P, TABLE_W], F32)
-            nc.gpsimd.iota(count_i[:], pattern=[[1, TABLE_W]], base=0, channel_multiplier=-1)
-            nc.vector.tensor_scalar(
-                out=dist[:], in0=count_i[:], scalar1=shift_col[:, 0:1], scalar2=None, op0=ALU.add
-            )
+            dist_i = setup_pool.tile([P, PRIOR_W], I32)
+            dist = setup_pool.tile([P, PRIOR_W], F32)
+            nc.gpsimd.iota(dist_i[:], pattern=[[1, PRIOR_W]], base=-(S - P), channel_multiplier=-1)
+            nc.vector.tensor_copy(out=dist[:], in_=dist_i[:])
 
-            work = [setup_pool.tile([P, TABLE_W], F32, name="work%d" % t) for t in range(TABLES)]
-            for t in range(TABLES):
-                nc.scalar.activation(out=work[t][:], in_=dist[:], func=ACT.Abs, bias=neg_offset[:, t : t + 1])
+            for which, rows_sb in ((0, q_sb), (1, k_sb)):
+                for pair in range(H // 2):
+                    qk_ps = banks.tile([P, 2, S], BF16, tag="bank")
+                    for i in range(2):
+                        head = slice(HD * (2 * pair + i), HD * (2 * pair + i + 1))
+                        for a in range(S_TILES):
+                            nc.tensor.transpose(qk_ps[:, i, P * a : P * (a + 1)], rows_sb[:, a, head], ident_bf[:])
+                    if which == 0:
+                        nc.scalar.copy(out=qk_t[:, which, 2 * pair : 2 * pair + 2, :], in_=qk_ps[:])
+                    else:
+                        nc.vector.tensor_copy(out=qk_t[:, which, 2 * pair : 2 * pair + 2, :], in_=qk_ps[:])
+            load_x(2)
+            load_w(2)
+            load_x(3)
+            load_w(3)
+            load_w(4)
+
+            work = setup_pool.tile([P, H, PRIOR_W], F32)
+            for h in range(H):
+                nc.scalar.activation(out=work[:, h, :], in_=dist[:], func=ACT.Abs, bias=neg_offset[:, h : h + 1])
                 nc.gpsimd.tensor_scalar(
-                    out=base[t][:],
-                    in0=work[t][:],
-                    scalar1=slope_col[:, t : t + 1],
+                    out=prior[:, h, :],
+                    in0=work[:, h, :],
+                    scalar1=slope[:, h : h + 1],
                     scalar2=EPS,
                     op0=ALU.mult,
                     op1=ALU.add,
                 )
-            for t in range(TABLES):
-                nc.scalar.activation(
-                    out=work[t][:], in_=work[t][:], func=ACT.Ln, scale=slope_col[:, t : t + 1], bias=eps_col[:, 0:1]
-                )
-            for t in range(TABLES):
-                nc.scalar.activation(out=work[t][:], in_=work[t][:], func=ACT.Exp, scale=root_col[:, t : t + 1])
-                for squaring in range(SQUARINGS):
-                    nc.scalar.activation(out=work[t][:], in_=work[t][:], func=ACT.Square)
-                nc.gpsimd.tensor_tensor(out=base[t][:], in0=base[t][:], in1=work[t][:], op=ALU.mult)
-
-        score_pool = ctx.enter_context(tc.tile_pool(name="score_pool", bufs=4, reuse_waits="tile"))
-        v_pool = ctx.enter_context(tc.tile_pool(name="v_pool", bufs=1, reuse_waits="tile"))
-        o_pool = ctx.enter_context(tc.tile_pool(name="o_pool", bufs=3, reuse_waits="tile"))
-
-        x_grouped = {}
-
-        def spread_prior():
-            for t in range(TABLES):
-                heads = slice(TABLE_HEADS * t, TABLE_HEADS * (t + 1))
-                nc.sync.dma_start(out=scratch[heads].rearrange("h r x -> (h r) x"), in_=base[t][:])
-            for t in range(TABLES):
-                heads = slice(TABLE_HEADS * t, TABLE_HEADS * (t + 1))
-                for j in range(P // TABLE_ROWS):
-                    first = P - TABLE_ROWS - TABLE_ROWS * j
-                    nc.sync.dma_start(
-                        out=prior[TABLE_ROWS * j : TABLE_ROWS * (j + 1), heads, :],
-                        in_=scratch[heads].rearrange("h r x -> r h x")[:, :, first : first + PRIOR_W],
-                    )
             for h in range(H):
-                nc.gpsimd.tensor_tensor(
-                    out=diag[:, h],
-                    in0=prior[:, h, S - P : S].unsqueeze(1).to_broadcast([P, S_TILES, P]),
-                    in1=mask_diag[:],
-                    op=ALU.subtract,
+                nc.scalar.activation(
+                    out=work[:, h, :], in_=work[:, h, :], func=ACT.Ln, scale=slope[:, h : h + 1], bias=eps_col[:, 0:1]
                 )
+            for pair in range(H // 2):
+                heads = (2 * pair, 2 * pair + 1)
+                for h in heads:
+                    nc.scalar.activation(out=work[:, h, :], in_=work[:, h, :], func=ACT.Exp, scale=root[:, h : h + 1])
+                for squaring in range(SQUARINGS):
+                    for h in heads:
+                        nc.scalar.activation(out=work[:, h, :], in_=work[:, h, :], func=ACT.Square)
+                for h in heads:
+                    nc.gpsimd.tensor_tensor(out=prior[:, h, :], in0=prior[:, h, :], in1=work[:, h, :], op=ALU.mult)
+                for h in heads:
+                    nc.gpsimd.tensor_tensor(
+                        out=diag[:, h],
+                        in0=prior[:, h, S - P : S].unsqueeze(1).to_broadcast([P, S_TILES, P]),
+                        in1=mask_diag[:],
+                        op=ALU.subtract,
+                    )
+
+        v_pool = ctx.enter_context(tc.tile_pool(name="v_pool", bufs=2, reuse_waits="tile"))
+        o_pool = ctx.enter_context(tc.tile_pool(name="o_pool", bufs=4, reuse_waits="tile"))
+        score_pool = ctx.enter_context(tc.tile_pool(name="score_pool", bufs=4, reuse_waits="tile"))
+
+        neg_s = {}
+        neg_max = {}
 
         def transpose_x(g):
             c, local = divmod(g, CHUNK_PASSES)
@@ -275,18 +254,13 @@ def tile_bayesianattention_pa_k_kernel(
                             ident_f32[:],
                         )
                 side_by_side = grouped_words[:, 2 * P * b : 2 * P * (b + 1), :]
-                if b == 1 and g >= SCALAR_JOINS:
+                if g >= FIRST_SCORE_SLOT:
                     nc.scalar.copy(out=side_by_side, in_=xt_ps[:].rearrange("p w s -> p s w"))
                 else:
                     nc.vector.tensor_copy(out=side_by_side, in_=xt_ps[:].rearrange("p w s -> p s w"))
-            x_grouped[g] = grouped
+            nc.vector.quantize_mx(out=x_codes[:, g, :].bitcast(FP8X4), scales=x_scales[:, g, :], in_=grouped[:])
             if local == CHUNK_PASSES - 1 and c + STREAM_BUFS < CHUNKS:
                 load_x(c + STREAM_BUFS)
-
-        def quantise_x(g):
-            nc.vector.quantize_mx(
-                out=x_codes[:, g, :].bitcast(FP8X4), scales=x_scales[:, g, :], in_=x_grouped[g][:]
-            )
 
         def project(v_ps, half, g):
             c, local = divmod(g, CHUNK_PASSES)
@@ -306,11 +280,9 @@ def tile_bayesianattention_pa_k_kernel(
             if local == CHUNK_PASSES - 1 and i + W_BUFS < HALVES * CHUNKS:
                 load_w(i + W_BUFS)
 
-        def score_tiles(first_tile, count):
-            tiles = [divmod(n, S_TILES) for n in range(first_tile, first_tile + count)]
+        def score_tiles(first_tile):
+            tiles = [divmod(n, S_TILES) for n in range(first_tile, first_tile + TILES_A_SLOT)]
             s_ps = {}
-            neg_s = {}
-            neg_max = {}
             for h, a in tiles:
                 s_ps[a] = banks.tile([P, S], F32, tag="bank", name="s_ps")
                 nc.tensor.matmul(
@@ -351,7 +323,9 @@ def tile_bayesianattention_pa_k_kernel(
                     op1=ALU.min,
                     accum_out=neg_max[a][:],
                 )
-            for h, a in tiles:
+
+        def exponentials(first_tile):
+            for h, a in [divmod(n, S_TILES) for n in range(first_tile, first_tile + TILES_A_SLOT)]:
                 nc.scalar.activation(
                     out=e_heads[h % 2][:, a, 0 : P * (a + 1)],
                     in_=neg_s[a][:, 0 : P * (a + 1)],
@@ -381,13 +355,16 @@ def tile_bayesianattention_pa_k_kernel(
                 out=e_codes[:, h, :].bitcast(FP8X4), scales=e_scales[:, h, :], in_=e_grouped[h % 2][:]
             )
 
-        def quantise_v(v_ps, half):
+        def round_v(sums):
             v_bf = v_pool.tile([P, S_TILES, HALF], BF16)
             for m in range(S_TILES):
                 if m % 2 == 0:
-                    nc.scalar.copy(out=v_bf[:, m, :], in_=v_ps[m][:])
+                    nc.scalar.copy(out=v_bf[:, m, :], in_=sums[m][:])
                 else:
-                    nc.vector.tensor_copy(out=v_bf[:, m, :], in_=v_ps[m][:])
+                    nc.vector.tensor_copy(out=v_bf[:, m, :], in_=sums[m][:])
+            return v_bf
+
+        def quantise_v(v_bf, half):
             grouped = v_pool.tile([P, HALF, S_TILES], BF16, align_bytes=64, name="v_grouped")
             nc.vector.tensor_copy(out=grouped[:], in_=v_bf[:].rearrange("p m n -> p n m"))
             nc.vector.quantize_mx(
@@ -417,48 +394,53 @@ def tile_bayesianattention_pa_k_kernel(
                     stop=True,
                 )
             o_sb = o_pool.tile([P, HALF_HEADS, HD], F32)
-            nc.vector.tensor_tensor(
-                out=o_sb[:],
-                in0=o_ps[:],
-                in1=inv_sum[:, a, :].unsqueeze(2).to_broadcast([P, HALF_HEADS, HD]),
-                op=ALU.mult,
-            )
+            if a % 2 == 0:
+                nc.vector.tensor_tensor(
+                    out=o_sb[:],
+                    in0=o_ps[:],
+                    in1=inv_sum[:, a, :].unsqueeze(2).to_broadcast([P, HALF_HEADS, HD]),
+                    op=ALU.mult,
+                )
+            else:
+                for i in range(HALF_HEADS):
+                    nc.scalar.activation(
+                        out=o_sb[:, i, :], in_=o_ps[:, i, :], func=ACT.Copy, scale=inv_sum[:, a, i : i + 1]
+                    )
             nc.sync.dma_start(
                 out=out_view[:, a, HALF * half : HALF * (half + 1)], in_=o_sb[:].rearrange("p h d -> p (h d)")
             )
 
-        v_ps = [v_psum.tile([P, HALF], F32, name="v_ps%d" % m, tag="v_ps%d" % m) for m in range(S_TILES)]
-        for g in range(PASSES + 1):
-            if g > 0:
-                quantise_x(g - 1)
-            if g < PASSES:
-                transpose_x(g)
-            if g > 0:
-                project(v_ps, 0, g - 1)
-            if g == SPREAD_PASS:
-                spread_prior()
-            if FIRST_SCORE_PASS <= g < PASSES:
-                score_tiles(TILES_A_PASS * (g - FIRST_SCORE_PASS), TILES_A_PASS)
-        quantise_v(v_ps, 0)
-
-        done_before = TILES_A_PASS * (PASSES - FIRST_SCORE_PASS)
-        first_attend = 2 * HALF_HEADS + 1
-        v_ps = [v_psum.tile([P, HALF], F32, name="v_ps%d" % m, tag="v_ps%d" % m) for m in range(S_TILES)]
-        for g in range(PASSES):
-            project(v_ps, 1, g)
-            if g == first_attend:
+        last_score_slot = FIRST_SCORE_SLOT + SCORE_TILES // TILES_A_SLOT - 1
+        first_attend = SLOTS + 1 - S_TILES
+        v_ps = {}
+        v_bf = {}
+        for t in range(SLOTS + 1):
+            after_scores = t - FIRST_SCORE_SLOT - HEAD_SLOTS - 2
+            if t < PASSES:
+                transpose_x(t)
+            if after_scores >= 0 and after_scores % HEAD_SLOTS == 0 and after_scores // HEAD_SLOTS < H:
+                transpose_e(after_scores // HEAD_SLOTS)
+            if after_scores >= 1 and after_scores % HEAD_SLOTS == 1 and after_scores // HEAD_SLOTS < H:
+                quantise_e(after_scores // HEAD_SLOTS)
+            if FIRST_SCORE_SLOT < t <= last_score_slot + 1:
+                exponentials(TILES_A_SLOT * (t - 1 - FIRST_SCORE_SLOT))
+            if FIRST_SCORE_SLOT <= t <= last_score_slot:
+                score_tiles(TILES_A_SLOT * (t - FIRST_SCORE_SLOT))
+            if t == first_attend - 1:
+                quantise_v(v_bf[0], 0)
                 inv_sum = invert_sums(0)
-            if first_attend <= g < first_attend + S_TILES:
-                attend(inv_sum, 0, g - first_attend)
-            if g % 2 == 1:
-                transpose_e(g // 2)
-            elif g > 0:
-                quantise_e(g // 2 - 1)
-            first_tile = done_before + TILES_A_PASS * g
-            if first_tile < SCORE_TILES:
-                score_tiles(first_tile, TILES_A_PASS)
-        quantise_e(H - 1)
-        quantise_v(v_ps, 1)
+            if t > 0:
+                half, g = divmod(t - 1, PASSES)
+                if g == 0:
+                    v_ps[half] = [
+                        v_psum.tile([P, HALF], F32, name="v_ps%d" % m, tag="v_ps%d" % m) for m in range(S_TILES)
+                    ]
+                project(v_ps[half], half, g)
+                if g == PASSES - 1:
+                    v_bf[half] = round_v(v_ps[half])
+            if t >= first_attend:
+                attend(inv_sum, 0, t - first_attend)
         inv_sum = invert_sums(1)
+        quantise_v(v_bf[1], 1)
         for a in range(S_TILES):
             attend(inv_sum, 1, a)

@@ -32,17 +32,21 @@ HALVES = E // HALF
 HALF_HEADS = HALF // HD
 PLANES = 4
 STREAM_BUFS = 4
+QK_BEHIND = 6
 W_BUFS = 5
+W_AHEAD = 3
 
 PRIOR_W = S
-SQUARINGS = 3
+CENTRE = math.log(64.0)
 EXP_HALVINGS = 10
 EXP_SERIES = (1.0, 1.0 / 2, 1.0 / 6, 1.0 / 24, 1.0 / 120)
 EXP_PLAIN = 3
 
 SCORE_TILES = H * S_TILES
 SLOTS = HALVES * PASSES
+TABLE_SLOT = 2
 FIRST_SCORE_SLOT = 12
+PREPARE_SLOTS = 2
 TILES_A_SLOT = 2
 HEAD_SLOTS = S_TILES // TILES_A_SLOT
 
@@ -74,8 +78,8 @@ def tile_bayesianattention_pa_k_kernel(
         ident_bf = keep.tile([P, P], BF16)
         ident_f32 = keep.tile([P, P], F32)
         prior = keep.tile([P, H, PRIOR_W], F32)
-        mask_diag = keep.tile([P, S_TILES, P], BF16)
-        diag = keep.tile([P, H, S_TILES, P], F32)
+        work = keep.tile([P, H, PRIOR_W], F32)
+        mask_near = keep.tile([P, P], BF16)
         e_heads = [keep.tile([P, S_TILES, S], BF16, name="e_head%d" % i) for i in range(2)]
         e_grouped = [keep.tile([P, 4 * S], BF16, align_bytes=64, name="e_grouped%d" % i) for i in range(2)]
         qk_t = keep.tile([P, 2, H, S], BF16)
@@ -91,6 +95,7 @@ def tile_bayesianattention_pa_k_kernel(
 
         x_tiles = {}
         w_tiles = {}
+        qk_rows = {}
 
         def load_x(c):
             x_sb = stream.tile([P, S_TILES, CHUNK_K], BF16, tag="stream", name="x_sb")
@@ -99,6 +104,20 @@ def tile_bayesianattention_pa_k_kernel(
                     out=x_sb[:, 2 * u : 2 * u + 2, :], in_=x_view[u][:, :, CHUNK_K * c : CHUNK_K * (c + 1)]
                 )
             x_tiles[c] = x_sb
+            load_w(c)
+
+        def load_rows(which):
+            rows_sb = stream.tile([P, S_TILES, E], BF16, tag="stream", name="rows_sb")
+            nc.sync.dma_start(out=rows_sb[:], in_=(q_view, k_view)[which])
+            qk_rows[which] = rows_sb
+
+        def load_next(n):
+            if n < QK_BEHIND:
+                load_x(n)
+            elif n < QK_BEHIND + 2:
+                load_rows(n - QK_BEHIND)
+            elif n < CHUNKS + 2:
+                load_x(n - 2)
 
         def load_w(i):
             half, c = divmod(i, CHUNKS)
@@ -122,121 +141,104 @@ def tile_bayesianattention_pa_k_kernel(
         make_identity(nc, ident_bf[:])
         make_identity(nc, ident_f32[:])
 
-        with tc.tile_pool(name="setup", bufs=1) as setup_pool:
-            scale_bf = setup_pool.tile([P, H], BF16)
-            loc_bf = setup_pool.tile([P, H], BF16)
-            shape_bf = setup_pool.tile([P, H], BF16)
-            nc.sync.dma_start(out=scale_bf[:], in_=scale.rearrange("a h b c -> (a h b c)").partition_broadcast(P))
-            nc.sync.dma_start(out=loc_bf[:], in_=loc.rearrange("a h b c -> (a h b c)").partition_broadcast(P))
-            nc.sync.dma_start(out=shape_bf[:], in_=shape.rearrange("a h b c -> (a h b c)").partition_broadcast(P))
-
-            q_sb = stream.tile([P, S_TILES, E], BF16, tag="stream")
-            k_sb = stream.tile([P, S_TILES, E], BF16, tag="stream")
-            nc.sync.dma_start(out=q_sb[:], in_=q_view)
-            nc.sync.dma_start(out=k_sb[:], in_=k_view)
-            load_x(0)
-            load_w(0)
-            load_x(1)
-            load_w(1)
-            for a in range(S_TILES):
-                nc.sync.dma_start(out=mask_diag[:, a, :], in_=mask_view[:, a, P * a : P * (a + 1)])
+        scale_bf = keep.tile([P, H], BF16)
+        loc_bf = keep.tile([P, H], BF16)
+        shape_bf = keep.tile([P, H], BF16)
+        nc.sync.dma_start(out=scale_bf[:], in_=scale.rearrange("a h b c -> (a h b c)").partition_broadcast(P))
+        nc.sync.dma_start(out=loc_bf[:], in_=loc.rearrange("a h b c -> (a h b c)").partition_broadcast(P))
+        nc.sync.dma_start(out=shape_bf[:], in_=shape.rearrange("a h b c -> (a h b c)").partition_broadcast(P))
+        for n in range(STREAM_BUFS):
+            load_next(n)
+        nc.sync.dma_start(out=mask_near[:], in_=mask_view[:, 0, 0:P])
 
 
-            exponent = setup_pool.tile([P, 3, H], F32)
-            eps_col = setup_pool.tile([P, 1], F32)
-            nc.vector.memset(eps_col[:], EPS)
-            nc.vector.tensor_copy(out=exponent[:, 0, :], in_=scale_bf[:])
-            nc.vector.tensor_copy(out=exponent[:, 1, :], in_=loc_bf[:])
-            nc.vector.tensor_scalar_mul(out=exponent[:, 2, :], in0=loc_bf[:], scalar1=-1.0)
+        kappa = keep.tile([P, H], F32)
+        neg_centre = keep.tile([P, H], F32)
+        exponent = keep.tile([P, 4, H], F32)
+        eps_col = keep.tile([P, 1], F32)
+        nc.vector.memset(eps_col[:], EPS)
+        nc.vector.tensor_scalar_add(out=kappa[:], in0=shape_bf[:], scalar1=-1.0)
+        nc.vector.tensor_copy(out=exponent[:, 0, :], in_=scale_bf[:])
+        nc.vector.tensor_copy(out=exponent[:, 1, :], in_=loc_bf[:])
+        nc.vector.tensor_scalar_mul(out=exponent[:, 2, :], in0=loc_bf[:], scalar1=-1.0)
+        nc.vector.tensor_scalar_mul(out=exponent[:, 3, :], in0=kappa[:], scalar1=CENTRE)
+        nc.vector.tensor_scalar_mul(out=neg_centre[:], in0=kappa[:], scalar1=-CENTRE)
 
-            small = setup_pool.tile([P, 3, H], F32)
-            grown = setup_pool.tile([P, 3, H], F32)
-            nc.vector.tensor_scalar_mul(out=small[:], in0=exponent[:], scalar1=1.0 / 2**EXP_HALVINGS)
-            nc.vector.tensor_scalar_mul(out=grown[:], in0=small[:], scalar1=EXP_SERIES[-1])
-            for coefficient in reversed(EXP_SERIES[:-1]):
-                nc.vector.scalar_tensor_tensor(
-                    out=grown[:], in0=grown[:], scalar=coefficient, in1=small[:], op0=ALU.add, op1=ALU.mult
-                )
-            for squaring in range(EXP_HALVINGS - EXP_PLAIN):
-                nc.vector.scalar_tensor_tensor(
-                    out=grown[:], in0=grown[:], scalar=2.0, in1=grown[:], op0=ALU.add, op1=ALU.mult
-                )
-            nc.vector.tensor_scalar_add(out=grown[:], in0=grown[:], scalar1=1.0)
-            for squaring in range(EXP_PLAIN):
-                nc.vector.tensor_mul(out=grown[:], in0=grown[:], in1=grown[:])
-            slope = grown[:, 0, :]
-            neg_offset = setup_pool.tile([P, H], F32)
-            nc.vector.tensor_sub(out=neg_offset[:], in0=grown[:, 2, :], in1=grown[:, 1, :])
-            root = setup_pool.tile([P, H], F32)
-            nc.vector.tensor_scalar(
-                out=root[:],
-                in0=shape_bf[:],
-                scalar1=1.0,
-                scalar2=1.0 / 2**SQUARINGS,
-                op0=ALU.subtract,
-                op1=ALU.mult,
+        small = keep.tile([P, 4, H], F32)
+        grown = keep.tile([P, 4, H], F32)
+        nc.vector.tensor_scalar_mul(out=small[:], in0=exponent[:], scalar1=1.0 / 2**EXP_HALVINGS)
+        nc.vector.tensor_scalar_mul(out=grown[:], in0=small[:], scalar1=EXP_SERIES[-1])
+        for coefficient in reversed(EXP_SERIES[:-1]):
+            nc.vector.scalar_tensor_tensor(
+                out=grown[:], in0=grown[:], scalar=coefficient, in1=small[:], op0=ALU.add, op1=ALU.mult
             )
+        for squaring in range(EXP_HALVINGS - EXP_PLAIN):
+            nc.vector.scalar_tensor_tensor(
+                out=grown[:], in0=grown[:], scalar=2.0, in1=grown[:], op0=ALU.add, op1=ALU.mult
+            )
+        nc.vector.tensor_scalar_add(out=grown[:], in0=grown[:], scalar1=1.0)
+        for squaring in range(EXP_PLAIN):
+            nc.vector.tensor_mul(out=grown[:], in0=grown[:], in1=grown[:])
+        slope = grown[:, 0, :]
+        neg_offset = keep.tile([P, H], F32)
+        slope_lift = keep.tile([P, H], F32)
+        eps_lift = keep.tile([P, H], F32)
+        nc.vector.tensor_sub(out=neg_offset[:], in0=grown[:, 2, :], in1=grown[:, 1, :])
+        nc.vector.tensor_mul(out=slope_lift[:], in0=grown[:, 0, :], in1=grown[:, 3, :])
+        nc.vector.tensor_scalar_mul(out=eps_lift[:], in0=grown[:, 3, :], scalar1=EPS)
 
-            dist_i = setup_pool.tile([P, PRIOR_W], I32)
-            dist = setup_pool.tile([P, PRIOR_W], F32)
-            nc.gpsimd.iota(dist_i[:], pattern=[[1, PRIOR_W]], base=-(S - P), channel_multiplier=-1)
-            nc.vector.tensor_copy(out=dist[:], in_=dist_i[:])
+        dist_i = keep.tile([P, PRIOR_W], I32)
+        dist = keep.tile([P, PRIOR_W], F32)
+        nc.gpsimd.iota(dist_i[:], pattern=[[1, PRIOR_W]], base=-(S - P), channel_multiplier=-1)
+        nc.vector.tensor_copy(out=dist[:], in_=dist_i[:])
 
-            for which, rows_sb in ((0, q_sb), (1, k_sb)):
-                for pair in range(H // 2):
-                    qk_ps = banks.tile([P, 2, S], BF16, tag="bank")
-                    for i in range(2):
-                        head = slice(HD * (2 * pair + i), HD * (2 * pair + i + 1))
-                        for a in range(S_TILES):
-                            nc.tensor.transpose(qk_ps[:, i, P * a : P * (a + 1)], rows_sb[:, a, head], ident_bf[:])
-                    if which == 0:
-                        nc.scalar.copy(out=qk_t[:, which, 2 * pair : 2 * pair + 2, :], in_=qk_ps[:])
-                    else:
-                        nc.vector.tensor_copy(out=qk_t[:, which, 2 * pair : 2 * pair + 2, :], in_=qk_ps[:])
-            load_x(2)
-            load_w(2)
-            load_x(3)
-            load_w(3)
-            load_w(4)
-
-            work = setup_pool.tile([P, H, PRIOR_W], F32)
-            for h in range(H):
-                nc.scalar.activation(out=work[:, h, :], in_=dist[:], func=ACT.Abs, bias=neg_offset[:, h : h + 1])
-                nc.gpsimd.tensor_scalar(
-                    out=prior[:, h, :],
-                    in0=work[:, h, :],
-                    scalar1=slope[:, h : h + 1],
-                    scalar2=EPS,
-                    op0=ALU.mult,
-                    op1=ALU.add,
-                )
+        def start_tables():
+            for pair in range(H // 2):
+                heads = (2 * pair, 2 * pair + 1)
+                for h in heads:
+                    nc.scalar.activation(out=work[:, h, :], in_=dist[:], func=ACT.Abs, bias=neg_offset[:, h : h + 1])
+                for h in heads:
+                    nc.scalar.activation(
+                        out=prior[:, h, :],
+                        in_=work[:, h, :],
+                        func=ACT.Identity,
+                        scale=slope_lift[:, h : h + 1],
+                        bias=eps_lift[:, h : h + 1],
+                    )
             for h in range(H):
                 nc.scalar.activation(
                     out=work[:, h, :], in_=work[:, h, :], func=ACT.Ln, scale=slope[:, h : h + 1], bias=eps_col[:, 0:1]
                 )
-            for pair in range(H // 2):
-                heads = (2 * pair, 2 * pair + 1)
-                for h in heads:
-                    nc.scalar.activation(out=work[:, h, :], in_=work[:, h, :], func=ACT.Exp, scale=root[:, h : h + 1])
-                for squaring in range(SQUARINGS):
-                    for h in heads:
-                        nc.scalar.activation(out=work[:, h, :], in_=work[:, h, :], func=ACT.Square)
-                for h in heads:
-                    nc.gpsimd.tensor_tensor(out=prior[:, h, :], in0=prior[:, h, :], in1=work[:, h, :], op=ALU.mult)
-                for h in heads:
-                    nc.gpsimd.tensor_tensor(
-                        out=diag[:, h],
-                        in0=prior[:, h, S - P : S].unsqueeze(1).to_broadcast([P, S_TILES, P]),
-                        in1=mask_diag[:],
-                        op=ALU.subtract,
-                    )
+            for h in range(H):
+                nc.scalar.activation(
+                    out=work[:, h, :],
+                    in_=work[:, h, :],
+                    func=ACT.Exp,
+                    scale=kappa[:, h : h + 1],
+                    bias=neg_centre[:, h : h + 1],
+                )
 
-        v_pool = ctx.enter_context(tc.tile_pool(name="v_pool", bufs=2, reuse_waits="tile"))
-        o_pool = ctx.enter_context(tc.tile_pool(name="o_pool", bufs=4, reuse_waits="tile"))
-        score_pool = ctx.enter_context(tc.tile_pool(name="score_pool", bufs=4, reuse_waits="tile"))
+        def finish_tables(heads):
+            for h in heads:
+                nc.vector.tensor_mul(out=prior[:, h, :], in0=prior[:, h, :], in1=work[:, h, :])
+            for h in heads:
+                nc.vector.tensor_sub(out=prior[:, h, S - P : S], in0=prior[:, h, S - P : S], in1=mask_near[:])
+
+        v_pool = ctx.enter_context(tc.tile_pool(name="v_pool", bufs=2))
+        o_pool = ctx.enter_context(tc.tile_pool(name="o_pool", bufs=4))
+        score_pool = ctx.enter_context(tc.tile_pool(name="score_pool", bufs=4))
 
         neg_s = {}
         neg_max = {}
+
+        def transpose_rows(which):
+            for pair in range(H // 2):
+                qk_ps = banks.tile([P, 2, S], BF16, tag="bank")
+                for i in range(2):
+                    head = slice(HD * (2 * pair + i), HD * (2 * pair + i + 1))
+                    for a in range(S_TILES):
+                        nc.tensor.transpose(qk_ps[:, i, P * a : P * (a + 1)], qk_rows[which][:, a, head], ident_bf[:])
+                nc.scalar.copy(out=qk_t[:, which, 2 * pair : 2 * pair + 2, :], in_=qk_ps[:])
 
         def transpose_x(g):
             c, local = divmod(g, CHUNK_PASSES)
@@ -254,13 +256,13 @@ def tile_bayesianattention_pa_k_kernel(
                             ident_f32[:],
                         )
                 side_by_side = grouped_words[:, 2 * P * b : 2 * P * (b + 1), :]
-                if g >= FIRST_SCORE_SLOT:
+                if g < TABLE_SLOT or g >= FIRST_SCORE_SLOT - PREPARE_SLOTS:
                     nc.scalar.copy(out=side_by_side, in_=xt_ps[:].rearrange("p w s -> p s w"))
                 else:
                     nc.vector.tensor_copy(out=side_by_side, in_=xt_ps[:].rearrange("p w s -> p s w"))
             nc.vector.quantize_mx(out=x_codes[:, g, :].bitcast(FP8X4), scales=x_scales[:, g, :], in_=grouped[:])
-            if local == CHUNK_PASSES - 1 and c + STREAM_BUFS < CHUNKS:
-                load_x(c + STREAM_BUFS)
+            if local == CHUNK_PASSES - 1:
+                load_next(c + STREAM_BUFS)
 
         def project(v_ps, half, g):
             c, local = divmod(g, CHUNK_PASSES)
@@ -277,8 +279,8 @@ def tile_bayesianattention_pa_k_kernel(
                     start=(g == 0),
                     stop=(g == PASSES - 1),
                 )
-            if local == CHUNK_PASSES - 1 and i + W_BUFS < HALVES * CHUNKS:
-                load_w(i + W_BUFS)
+            if local == CHUNK_PASSES - 1 and CHUNKS <= i + W_AHEAD < HALVES * CHUNKS:
+                load_w(i + W_AHEAD)
 
         def score_tiles(first_tile):
             tiles = [divmod(n, S_TILES) for n in range(first_tile, first_tile + TILES_A_SLOT)]
@@ -294,24 +296,14 @@ def tile_bayesianattention_pa_k_kernel(
                 )
             for h, a in tiles:
                 neg_s[a] = score_pool.tile([P, S], F32, name="neg_s")
-                own = slice(P * a, P * (a + 1))
                 nc.vector.scalar_tensor_tensor(
-                    out=neg_s[a][:, own],
-                    in0=s_ps[a][:, own],
+                    out=neg_s[a][:, 0 : P * (a + 1)],
+                    in0=s_ps[a][:, 0 : P * (a + 1)],
                     scalar=-1.0 / math.sqrt(HD),
-                    in1=diag[:, h, a, :],
+                    in1=prior[:, h, S - P * (a + 1) : S],
                     op0=ALU.mult,
                     op1=ALU.add,
                 )
-                if a > 0:
-                    nc.vector.scalar_tensor_tensor(
-                        out=neg_s[a][:, 0 : P * a],
-                        in0=s_ps[a][:, 0 : P * a],
-                        scalar=-1.0 / math.sqrt(HD),
-                        in1=prior[:, h, S - P - P * a : S - P],
-                        op0=ALU.mult,
-                        op1=ALU.add,
-                    )
             for h, a in tiles:
                 neg_max[a] = score_pool.tile([P, 1], F32, name="neg_max")
                 nc.vector.tensor_scalar(
@@ -365,7 +357,7 @@ def tile_bayesianattention_pa_k_kernel(
             return v_bf
 
         def quantise_v(v_bf, half):
-            grouped = v_pool.tile([P, HALF, S_TILES], BF16, align_bytes=64, name="v_grouped")
+            grouped = v_pool.tile([P, HALF, S_TILES], BF16, align_bytes=64, name="v_grouped", bufs=1)
             nc.vector.tensor_copy(out=grouped[:], in_=v_bf[:].rearrange("p m n -> p n m"))
             nc.vector.quantize_mx(
                 out=v_codes[:, half, :].bitcast(FP8X4),
@@ -418,6 +410,12 @@ def tile_bayesianattention_pa_k_kernel(
             after_scores = t - FIRST_SCORE_SLOT - HEAD_SLOTS - 2
             if t < PASSES:
                 transpose_x(t)
+            if t == TABLE_SLOT:
+                start_tables()
+            prepare = t - (FIRST_SCORE_SLOT - PREPARE_SLOTS)
+            if 0 <= prepare < PREPARE_SLOTS:
+                transpose_rows(prepare)
+                finish_tables(range(H // PREPARE_SLOTS * prepare, H // PREPARE_SLOTS * (prepare + 1)))
             if after_scores >= 0 and after_scores % HEAD_SLOTS == 0 and after_scores // HEAD_SLOTS < H:
                 transpose_e(after_scores // HEAD_SLOTS)
             if after_scores >= 1 and after_scores % HEAD_SLOTS == 1 and after_scores // HEAD_SLOTS < H:

@@ -44,7 +44,6 @@ EXP_PLAIN = 3
 
 SCORE_TILES = H * S_TILES
 SLOTS = HALVES * PASSES
-TABLE_SLOT = 2
 FIRST_SCORE_SLOT = 12
 PREPARE_SLOTS = 2
 TILES_A_SLOT = 2
@@ -138,7 +137,6 @@ def tile_bayesianattention_pa_k_kernel(
         for i in range(2):
             nc.vector.memset(e_heads[i][:].rearrange("p a j -> p (a j)").bitcast(I32), 0)
             nc.vector.memset(e_grouped[i][:].bitcast(I32), 0)
-        make_identity(nc, ident_bf[:])
         make_identity(nc, ident_f32[:])
 
         scale_bf = keep.tile([P, H], BF16)
@@ -154,69 +152,75 @@ def tile_bayesianattention_pa_k_kernel(
 
         kappa = keep.tile([P, H], F32)
         neg_centre = keep.tile([P, H], F32)
-        exponent = keep.tile([P, 4, H], F32)
         eps_col = keep.tile([P, 1], F32)
         nc.vector.memset(eps_col[:], EPS)
         nc.vector.tensor_scalar_add(out=kappa[:], in0=shape_bf[:], scalar1=-1.0)
-        nc.vector.tensor_copy(out=exponent[:, 0, :], in_=scale_bf[:])
-        nc.vector.tensor_copy(out=exponent[:, 1, :], in_=loc_bf[:])
-        nc.vector.tensor_scalar_mul(out=exponent[:, 2, :], in0=loc_bf[:], scalar1=-1.0)
-        nc.vector.tensor_scalar_mul(out=exponent[:, 3, :], in0=kappa[:], scalar1=CENTRE)
         nc.vector.tensor_scalar_mul(out=neg_centre[:], in0=kappa[:], scalar1=-CENTRE)
-
-        small = keep.tile([P, 4, H], F32)
-        grown = keep.tile([P, 4, H], F32)
-        nc.vector.tensor_scalar_mul(out=small[:], in0=exponent[:], scalar1=1.0 / 2**EXP_HALVINGS)
-        nc.vector.tensor_scalar_mul(out=grown[:], in0=small[:], scalar1=EXP_SERIES[-1])
-        for coefficient in reversed(EXP_SERIES[:-1]):
-            nc.vector.scalar_tensor_tensor(
-                out=grown[:], in0=grown[:], scalar=coefficient, in1=small[:], op0=ALU.add, op1=ALU.mult
-            )
-        for squaring in range(EXP_HALVINGS - EXP_PLAIN):
-            nc.vector.scalar_tensor_tensor(
-                out=grown[:], in0=grown[:], scalar=2.0, in1=grown[:], op0=ALU.add, op1=ALU.mult
-            )
-        nc.vector.tensor_scalar_add(out=grown[:], in0=grown[:], scalar1=1.0)
-        for squaring in range(EXP_PLAIN):
-            nc.vector.tensor_mul(out=grown[:], in0=grown[:], in1=grown[:])
-        slope = grown[:, 0, :]
+        slope = keep.tile([P, H], F32)
+        exp_loc = keep.tile([P, H], F32)
+        exp_neg_loc = keep.tile([P, H], F32)
+        lift = keep.tile([P, H], F32)
+        nc.scalar.activation(out=exp_loc[:], in_=loc_bf[:], func=ACT.Exp)
+        nc.scalar.activation(out=exp_neg_loc[:], in_=loc_bf[:], func=ACT.Exp, scale=-1.0)
+        nc.scalar.activation(out=slope[:], in_=scale_bf[:], func=ACT.Exp)
+        nc.scalar.activation(out=lift[:], in_=kappa[:], func=ACT.Exp, scale=CENTRE)
         neg_offset = keep.tile([P, H], F32)
-        slope_lift = keep.tile([P, H], F32)
         eps_lift = keep.tile([P, H], F32)
-        nc.vector.tensor_sub(out=neg_offset[:], in0=grown[:, 2, :], in1=grown[:, 1, :])
-        nc.vector.tensor_mul(out=slope_lift[:], in0=grown[:, 0, :], in1=grown[:, 3, :])
-        nc.vector.tensor_scalar_mul(out=eps_lift[:], in0=grown[:, 3, :], scalar1=EPS)
+        nc.vector.tensor_sub(out=neg_offset[:], in0=exp_neg_loc[:], in1=exp_loc[:])
+        nc.vector.tensor_scalar_mul(out=eps_lift[:], in0=lift[:], scalar1=EPS)
 
         dist_i = keep.tile([P, PRIOR_W], I32)
         dist = keep.tile([P, PRIOR_W], F32)
         nc.gpsimd.iota(dist_i[:], pattern=[[1, PRIOR_W]], base=-(S - P), channel_multiplier=-1)
         nc.vector.tensor_copy(out=dist[:], in_=dist_i[:])
 
-        def start_tables():
-            for pair in range(H // 2):
-                heads = (2 * pair, 2 * pair + 1)
-                for h in heads:
-                    nc.scalar.activation(out=work[:, h, :], in_=dist[:], func=ACT.Abs, bias=neg_offset[:, h : h + 1])
-                for h in heads:
-                    nc.scalar.activation(
-                        out=prior[:, h, :],
-                        in_=work[:, h, :],
-                        func=ACT.Identity,
-                        scale=slope_lift[:, h : h + 1],
-                        bias=eps_lift[:, h : h + 1],
-                    )
-            for h in range(H):
-                nc.scalar.activation(
-                    out=work[:, h, :], in_=work[:, h, :], func=ACT.Ln, scale=slope[:, h : h + 1], bias=eps_col[:, 0:1]
-                )
-            for h in range(H):
-                nc.scalar.activation(
-                    out=work[:, h, :],
-                    in_=work[:, h, :],
-                    func=ACT.Exp,
-                    scale=kappa[:, h : h + 1],
-                    bias=neg_centre[:, h : h + 1],
-                )
+        small = keep.tile([P, H], F32)
+        grown = keep.tile([P, H], F32)
+        plus = keep.tile([P, H], F32)
+        nc.gpsimd.tensor_scalar(
+            out=plus[:], in0=shape_bf[:], scalar1=CENTRE, scalar2=-CENTRE, op0=ALU.mult, op1=ALU.add
+        )
+        nc.gpsimd.tensor_tensor(out=small[:], in0=plus[:], in1=scale_bf[:], op=ALU.add)
+
+        def scale_and_add(out, in0, factor, term):
+            nc.gpsimd.tensor_scalar(out=out, in0=in0, scalar1=factor, scalar2=term, op0=ALU.mult, op1=ALU.add)
+
+        scale_and_add(small[:], small[:], 1.0 / 2**EXP_HALVINGS, 0.0)
+        scale_and_add(grown[:], small[:], EXP_SERIES[-1], 0.0)
+        for coefficient in reversed(EXP_SERIES[:-1]):
+            scale_and_add(plus[:], grown[:], 1.0, coefficient)
+            nc.gpsimd.tensor_tensor(out=grown[:], in0=plus[:], in1=small[:], op=ALU.mult)
+        for squaring in range(EXP_HALVINGS - EXP_PLAIN):
+            scale_and_add(plus[:], grown[:], 1.0, 2.0)
+            nc.gpsimd.tensor_tensor(out=grown[:], in0=plus[:], in1=grown[:], op=ALU.mult)
+        scale_and_add(grown[:], grown[:], 1.0, 1.0)
+        for squaring in range(EXP_PLAIN):
+            nc.gpsimd.tensor_tensor(out=grown[:], in0=grown[:], in1=grown[:], op=ALU.mult)
+        slope_lift = grown
+        make_identity(nc, ident_bf[:])
+
+        for h in range(H):
+            nc.scalar.activation(out=work[:, h, :], in_=dist[:], func=ACT.Abs, bias=neg_offset[:, h : h + 1])
+        for h in range(H):
+            nc.scalar.activation(
+                out=prior[:, h, :], in_=work[:, h, :], func=ACT.Ln, scale=slope[:, h : h + 1], bias=eps_col[:, 0:1]
+            )
+        for h in range(H):
+            nc.scalar.activation(
+                out=prior[:, h, :],
+                in_=prior[:, h, :],
+                func=ACT.Exp,
+                scale=kappa[:, h : h + 1],
+                bias=neg_centre[:, h : h + 1],
+            )
+        for h in range(H):
+            nc.scalar.activation(
+                out=work[:, h, :],
+                in_=work[:, h, :],
+                func=ACT.Identity,
+                scale=slope_lift[:, h : h + 1],
+                bias=eps_lift[:, h : h + 1],
+            )
 
         def finish_tables(heads):
             for h in heads:
@@ -224,7 +228,7 @@ def tile_bayesianattention_pa_k_kernel(
             for h in heads:
                 nc.vector.tensor_sub(out=prior[:, h, S - P : S], in0=prior[:, h, S - P : S], in1=mask_near[:])
 
-        v_pool = ctx.enter_context(tc.tile_pool(name="v_pool", bufs=2))
+        v_pool = ctx.enter_context(tc.tile_pool(name="v_pool", bufs=1))
         o_pool = ctx.enter_context(tc.tile_pool(name="o_pool", bufs=4))
         score_pool = ctx.enter_context(tc.tile_pool(name="score_pool", bufs=4))
 
@@ -256,7 +260,7 @@ def tile_bayesianattention_pa_k_kernel(
                             ident_f32[:],
                         )
                 side_by_side = grouped_words[:, 2 * P * b : 2 * P * (b + 1), :]
-                if g < TABLE_SLOT or g >= FIRST_SCORE_SLOT - PREPARE_SLOTS:
+                if g >= FIRST_SCORE_SLOT - PREPARE_SLOTS:
                     nc.scalar.copy(out=side_by_side, in_=xt_ps[:].rearrange("p w s -> p s w"))
                 else:
                     nc.vector.tensor_copy(out=side_by_side, in_=xt_ps[:].rearrange("p w s -> p s w"))
@@ -356,9 +360,15 @@ def tile_bayesianattention_pa_k_kernel(
                     nc.vector.tensor_copy(out=v_bf[:, m, :], in_=sums[m][:])
             return v_bf
 
-        def quantise_v(v_bf, half):
-            grouped = v_pool.tile([P, HALF, S_TILES], BF16, align_bytes=64, name="v_grouped", bufs=1)
-            nc.vector.tensor_copy(out=grouped[:], in_=v_bf[:].rearrange("p m n -> p n m"))
+        def group_v(rounded, half):
+            grouped = v_pool.tile([P, HALF, S_TILES], BF16, align_bytes=64, name="v_grouped", bufs=2)
+            if half == 0:
+                scale_and_add(grouped[:], rounded[:].rearrange("p m n -> p n m"), 1.0, 0.0)
+            else:
+                nc.vector.tensor_copy(out=grouped[:], in_=rounded[:].rearrange("p m n -> p n m"))
+            return grouped
+
+        def quantise_v(grouped, half):
             nc.vector.quantize_mx(
                 out=v_codes[:, half, :].bitcast(FP8X4),
                 scales=v_scales[:, half, :],
@@ -366,7 +376,7 @@ def tile_bayesianattention_pa_k_kernel(
             )
 
         def invert_sums(half):
-            inv_sum = o_pool.tile([P, S_TILES, HALF_HEADS], F32)
+            inv_sum = o_pool.tile([P, S_TILES, HALF_HEADS], F32, name="inv_sum")
             nc.vector.reciprocal(out=inv_sum[:], in_=row_sum[:, :, HALF_HEADS * half : HALF_HEADS * (half + 1)])
             return inv_sum
 
@@ -405,13 +415,12 @@ def tile_bayesianattention_pa_k_kernel(
         last_score_slot = FIRST_SCORE_SLOT + SCORE_TILES // TILES_A_SLOT - 1
         first_attend = SLOTS + 1 - S_TILES
         v_ps = {}
-        v_bf = {}
+        v_grouped = {}
+        inv_sums = {}
         for t in range(SLOTS + 1):
             after_scores = t - FIRST_SCORE_SLOT - HEAD_SLOTS - 2
             if t < PASSES:
                 transpose_x(t)
-            if t == TABLE_SLOT:
-                start_tables()
             prepare = t - (FIRST_SCORE_SLOT - PREPARE_SLOTS)
             if 0 <= prepare < PREPARE_SLOTS:
                 transpose_rows(prepare)
@@ -424,9 +433,11 @@ def tile_bayesianattention_pa_k_kernel(
                 exponentials(TILES_A_SLOT * (t - 1 - FIRST_SCORE_SLOT))
             if FIRST_SCORE_SLOT <= t <= last_score_slot:
                 score_tiles(TILES_A_SLOT * (t - FIRST_SCORE_SLOT))
-            if t == first_attend - 1:
-                quantise_v(v_bf[0], 0)
-                inv_sum = invert_sums(0)
+            if t == first_attend - 2:
+                quantise_v(v_grouped[0], 0)
+                inv_sums[0] = invert_sums(0)
+            if t == last_score_slot + 2:
+                inv_sums[1] = invert_sums(1)
             if t > 0:
                 half, g = divmod(t - 1, PASSES)
                 if g == 0:
@@ -435,10 +446,9 @@ def tile_bayesianattention_pa_k_kernel(
                     ]
                 project(v_ps[half], half, g)
                 if g == PASSES - 1:
-                    v_bf[half] = round_v(v_ps[half])
+                    v_grouped[half] = group_v(round_v(v_ps[half]), half)
             if t >= first_attend:
-                attend(inv_sum, 0, t - first_attend)
-        inv_sum = invert_sums(1)
-        quantise_v(v_bf[1], 1)
+                attend(inv_sums[0], 0, t - first_attend)
+        quantise_v(v_grouped[1], 1)
         for a in range(S_TILES):
-            attend(inv_sum, 1, a)
+            attend(inv_sums[1], 1, a)

@@ -105,18 +105,23 @@ def tile_bayesianattention_pa_k_kernel(
             x_tiles[c] = x_sb
             load_w(c)
 
-        def load_rows(which):
-            rows_sb = stream.tile([P, S_TILES, E], BF16, tag="stream", name="rows_sb")
-            nc.sync.dma_start(out=rows_sb[:], in_=(q_view, k_view)[which])
-            qk_rows[which] = rows_sb
+        def load_rows(half):
+            rows_sb = stream.tile([P, 2, S_TILES, HALF], BF16, tag="stream", name="rows_sb")
+            for which in range(2):
+                nc.sync.dma_start(
+                    out=rows_sb[:, which, :, :], in_=(q_view, k_view)[which][:, :, HALF * half : HALF * (half + 1)]
+                )
+            qk_rows[half] = rows_sb
 
         def load_next(n):
             if n < QK_BEHIND:
                 load_x(n)
-            elif n < QK_BEHIND + 2:
-                load_rows(n - QK_BEHIND)
-            elif n < CHUNKS + 2:
-                load_x(n - 2)
+            elif n == QK_BEHIND:
+                load_rows(0)
+            elif n < CHUNKS + 1:
+                load_x(n - 1)
+            elif n == CHUNKS + 1:
+                load_rows(1)
 
         def load_w(i):
             half, c = divmod(i, CHUNKS)
@@ -235,14 +240,17 @@ def tile_bayesianattention_pa_k_kernel(
         neg_s = {}
         neg_max = {}
 
-        def transpose_rows(which):
-            for pair in range(H // 2):
+        def transpose_rows(half, which):
+            for pair in range(HALF_HEADS // 2):
                 qk_ps = banks.tile([P, 2, S], BF16, tag="bank")
                 for i in range(2):
                     head = slice(HD * (2 * pair + i), HD * (2 * pair + i + 1))
                     for a in range(S_TILES):
-                        nc.tensor.transpose(qk_ps[:, i, P * a : P * (a + 1)], qk_rows[which][:, a, head], ident_bf[:])
-                nc.scalar.copy(out=qk_t[:, which, 2 * pair : 2 * pair + 2, :], in_=qk_ps[:])
+                        nc.tensor.transpose(
+                            qk_ps[:, i, P * a : P * (a + 1)], qk_rows[half][:, which, a, head], ident_bf[:]
+                        )
+                first_head = HALF_HEADS * half + 2 * pair
+                nc.scalar.copy(out=qk_t[:, which, first_head : first_head + 2, :], in_=qk_ps[:])
 
         def transpose_x(g):
             c, local = divmod(g, CHUNK_PASSES)
@@ -423,8 +431,11 @@ def tile_bayesianattention_pa_k_kernel(
                 transpose_x(t)
             prepare = t - (FIRST_SCORE_SLOT - PREPARE_SLOTS)
             if 0 <= prepare < PREPARE_SLOTS:
-                transpose_rows(prepare)
+                transpose_rows(0, prepare)
                 finish_tables(range(H // PREPARE_SLOTS * prepare, H // PREPARE_SLOTS * (prepare + 1)))
+            prepare_late = prepare - HALF_HEADS * HEAD_SLOTS
+            if 0 <= prepare_late < PREPARE_SLOTS:
+                transpose_rows(1, prepare_late)
             if after_scores >= 0 and after_scores % HEAD_SLOTS == 0 and after_scores // HEAD_SLOTS < H:
                 transpose_e(after_scores // HEAD_SLOTS)
             if after_scores >= 1 and after_scores % HEAD_SLOTS == 1 and after_scores // HEAD_SLOTS < H:

@@ -35,6 +35,7 @@ STREAM_BUFS = 4
 QK_BEHIND = 6
 W_BUFS = 5
 W_AHEAD = 3
+V_PARTS = ((0, 512), (512, 256), (768, 256))
 
 PRIOR_W = S
 CENTRE = math.log(64.0)
@@ -48,6 +49,8 @@ FIRST_SCORE_SLOT = 12
 PREPARE_SLOTS = 2
 TILES_A_SLOT = 2
 HEAD_SLOTS = S_TILES // TILES_A_SLOT
+
+EV = {"quant0":27,"attend0":29,"group1":28,"quant1":29,"attend1":31,"inv2":30}
 
 FLOPS = 2 * S * D * E + 2 * 2 * H * S * S * HD
 
@@ -88,8 +91,9 @@ def tile_bayesianattention_pa_k_kernel(
         x_scales = keep.tile([P, PASSES, S], U8, align_bytes=64)
         e_codes = keep.tile([P, H, S], U32, align_bytes=64)
         e_scales = keep.tile([P, H, S], U8, align_bytes=64)
-        v_codes = keep.tile([P, HALVES, HALF], U32, align_bytes=64)
-        v_scales = keep.tile([P, HALVES, HALF], U8, align_bytes=64)
+        v_codes = keep.tile([P, E], U32, align_bytes=64)
+        v_scales = keep.tile([P, E], U8, align_bytes=64)
+        inv_sum = keep.tile([P, S_TILES, H], F32)
         planes_words = w_planes[:].bitcast(I32)
 
         x_tiles = {}
@@ -124,18 +128,17 @@ def tile_bayesianattention_pa_k_kernel(
                 load_rows(1)
 
         def load_w(i):
-            half, c = divmod(i, CHUNKS)
+            part, c = divmod(i, CHUNKS)
+            first, width = V_PARTS[part]
             first_pass = CHUNK_PASSES * c
-            if half == 0 and first_pass % PLANES == 0:
+            if part == 0 and first_pass % PLANES == 0:
                 for j in range(4):
                     nc.sync.dma_start(
                         out=planes_words[32 * j : 32 * j + 4 * PLANES, first_pass // PLANES, :],
                         in_=w_scale_view[first_pass : first_pass + PLANES, 4 * j : 4 * j + 4, :],
                     )
-            w_sb = w_pool.tile([P, CHUNK_PASSES, HALF], I32, align_bytes=64, name="w_sb")
-            nc.sync.dma_start(
-                out=w_sb[:], in_=w_view[:, first_pass : first_pass + CHUNK_PASSES, HALF * half : HALF * (half + 1)]
-            )
+            w_sb = w_pool.tile([P, CHUNK_PASSES, width], I32, align_bytes=64, name="w_sb")
+            nc.sync.dma_start(out=w_sb[:], in_=w_view[:, first_pass : first_pass + CHUNK_PASSES, first : first + width])
             w_tiles[i] = w_sb
 
         nc.vector.memset(w_planes[:].rearrange("p t n -> p (t n)").bitcast(I32), 0)
@@ -276,23 +279,36 @@ def tile_bayesianattention_pa_k_kernel(
             if local == CHUNK_PASSES - 1:
                 load_next(c + STREAM_BUFS)
 
-        def project(v_ps, half, g):
-            c, local = divmod(g, CHUNK_PASSES)
-            i = CHUNKS * half + c
-            plane = PLANES * (g % PLANES)
-            for m in range(S_TILES):
-                cols = slice(P * m, P * (m + 1))
-                nc.tensor.matmul_mx(
-                    out=v_ps[m][:],
-                    lhsT=x_codes[:, g, cols].bitcast(FP8X4),
-                    lhsT_scale=x_scales[:, g, cols],
-                    rhs=w_tiles[i][:, local, :].bitcast(FP8X4),
-                    rhs_scale=w_planes[plane:P, g // PLANES, HALF * half : HALF * (half + 1)],
-                    start=(g == 0),
-                    stop=(g == PASSES - 1),
-                )
-            if local == CHUNK_PASSES - 1 and CHUNKS <= i + W_AHEAD < HALVES * CHUNKS:
-                load_w(i + W_AHEAD)
+        def project(u):
+            if u < PASSES:
+                part, passes = 0, [u]
+            else:
+                part, c = 1 + (u - PASSES) // CHUNKS, (u - PASSES) % CHUNKS
+                passes = [CHUNK_PASSES * c, CHUNK_PASSES * c + 1]
+            first, width = V_PARTS[part]
+            if passes[0] == 0:
+                v_ps[part] = [
+                    v_psum.tile([P, width], F32, name="v_ps%d" % m, tag="v_ps%d" % m) for m in range(S_TILES)
+                ]
+            for g in passes:
+                c, local = divmod(g, CHUNK_PASSES)
+                i = CHUNKS * part + c
+                plane = PLANES * (g % PLANES)
+                for m in range(S_TILES):
+                    cols = slice(P * m, P * (m + 1))
+                    nc.tensor.matmul_mx(
+                        out=v_ps[part][m][:],
+                        lhsT=x_codes[:, g, cols].bitcast(FP8X4),
+                        lhsT_scale=x_scales[:, g, cols],
+                        rhs=w_tiles[i][:, local, :].bitcast(FP8X4),
+                        rhs_scale=w_planes[plane:P, g // PLANES, first : first + width],
+                        start=(g == 0),
+                        stop=(g == PASSES - 1),
+                    )
+                if local == CHUNK_PASSES - 1 and CHUNKS <= i + W_AHEAD < len(V_PARTS) * CHUNKS:
+                    load_w(i + W_AHEAD)
+            if passes[-1] == PASSES - 1:
+                round_v(part)
 
         def score_tiles(first_tile):
             tiles = [divmod(n, S_TILES) for n in range(first_tile, first_tile + TILES_A_SLOT)]
@@ -359,72 +375,77 @@ def tile_bayesianattention_pa_k_kernel(
                 out=e_codes[:, h, :].bitcast(FP8X4), scales=e_scales[:, h, :], in_=e_grouped[h % 2][:]
             )
 
-        def round_v(sums):
-            v_bf = v_pool.tile([P, S_TILES, HALF], BF16)
+        def round_v(part):
+            v_bf[part] = v_pool.tile([P, S_TILES, V_PARTS[part][1]], BF16, name="v_bf", bufs=2)
             for m in range(S_TILES):
                 if m % 2 == 0:
-                    nc.scalar.copy(out=v_bf[:, m, :], in_=sums[m][:])
+                    nc.scalar.copy(out=v_bf[part][:, m, :], in_=v_ps[part][m][:])
                 else:
-                    nc.vector.tensor_copy(out=v_bf[:, m, :], in_=sums[m][:])
-            return v_bf
+                    nc.vector.tensor_copy(out=v_bf[part][:, m, :], in_=v_ps[part][m][:])
 
-        def group_v(rounded, half):
-            grouped = v_pool.tile([P, HALF, S_TILES], BF16, align_bytes=64, name="v_grouped", bufs=2)
-            if half == 0:
-                scale_and_add(grouped[:], rounded[:].rearrange("p m n -> p n m"), 1.0, 0.0)
+        def group_v(part):
+            grouped = v_pool.tile([P, V_PARTS[part][1], S_TILES], BF16, align_bytes=64, name="v_grouped", bufs=2)
+            if part == 0:
+                scale_and_add(grouped[:], v_bf[part][:].rearrange("p m n -> p n m"), 1.0, 0.0)
             else:
-                nc.vector.tensor_copy(out=grouped[:], in_=rounded[:].rearrange("p m n -> p n m"))
-            return grouped
+                nc.vector.tensor_copy(out=grouped[:], in_=v_bf[part][:].rearrange("p m n -> p n m"))
+            v_grouped[part] = grouped
 
-        def quantise_v(grouped, half):
+        def quantise_v(part):
+            first, width = V_PARTS[part]
             nc.vector.quantize_mx(
-                out=v_codes[:, half, :].bitcast(FP8X4),
-                scales=v_scales[:, half, :],
-                in_=grouped[:].rearrange("p n m -> p (n m)"),
+                out=v_codes[:, first : first + width].bitcast(FP8X4),
+                scales=v_scales[:, first : first + width],
+                in_=v_grouped[part][:].rearrange("p n m -> p (n m)"),
             )
 
-        def invert_sums(half):
-            inv_sum = o_pool.tile([P, S_TILES, HALF_HEADS], F32, name="inv_sum")
-            nc.vector.reciprocal(out=inv_sum[:], in_=row_sum[:, :, HALF_HEADS * half : HALF_HEADS * (half + 1)])
-            return inv_sum
+        def invert_sums(part):
+            first, width = V_PARTS[part]
+            heads = slice(first // HD, (first + width) // HD)
+            nc.vector.reciprocal(out=inv_sum[:, :, heads], in_=row_sum[:, :, heads])
 
-        def attend(inv_sum, half, a):
-            rows = slice(P * a, P * (a + 1))
-            o_ps = banks.tile([P, HALF_HEADS, HD], F32, tag="bank")
-            for i in range(HALF_HEADS):
-                h = HALF_HEADS * half + i
-                cols = slice(HD * i, HD * (i + 1))
-                nc.tensor.matmul_mx(
-                    out=o_ps[:, i, :],
-                    lhsT=e_codes[:, h, rows].bitcast(FP8X4),
-                    lhsT_scale=e_scales[:, h, rows],
-                    rhs=v_codes[:, half, cols].bitcast(FP8X4),
-                    rhs_scale=v_scales[:, half, cols],
-                    start=True,
-                    stop=True,
-                )
-            o_sb = o_pool.tile([P, HALF_HEADS, HD], F32)
-            if a % 2 == 0:
+        def attend(part, i, on_vector):
+            first, width = V_PARTS[part]
+            heads = width // HD
+            tiles = HALF // width
+            first_head = first // HD
+            first_tile = tiles * i
+            o_ps = banks.tile([P, tiles, heads, HD], F32, tag="bank")
+            for a in range(tiles):
+                rows = slice(P * (first_tile + a), P * (first_tile + a + 1))
+                for j in range(heads):
+                    h = first_head + j
+                    cols = slice(HD * h, HD * (h + 1))
+                    nc.tensor.matmul_mx(
+                        out=o_ps[:, a, j, :],
+                        lhsT=e_codes[:, h, rows].bitcast(FP8X4),
+                        lhsT_scale=e_scales[:, h, rows],
+                        rhs=v_codes[:, cols].bitcast(FP8X4),
+                        rhs_scale=v_scales[:, cols],
+                        start=True,
+                        stop=True,
+                    )
+            o_sb = o_pool.tile([P, tiles, heads, HD], F32)
+            factors = inv_sum[:, first_tile : first_tile + tiles, first_head : first_head + heads]
+            if on_vector:
                 nc.vector.tensor_tensor(
-                    out=o_sb[:],
-                    in0=o_ps[:],
-                    in1=inv_sum[:, a, :].unsqueeze(2).to_broadcast([P, HALF_HEADS, HD]),
-                    op=ALU.mult,
+                    out=o_sb[:], in0=o_ps[:], in1=factors.unsqueeze(3).to_broadcast([P, tiles, heads, HD]), op=ALU.mult
                 )
             else:
-                for i in range(HALF_HEADS):
-                    nc.scalar.activation(
-                        out=o_sb[:, i, :], in_=o_ps[:, i, :], func=ACT.Copy, scale=inv_sum[:, a, i : i + 1]
-                    )
+                for a in range(tiles):
+                    for j in range(heads):
+                        nc.scalar.activation(
+                            out=o_sb[:, a, j, :], in_=o_ps[:, a, j, :], func=ACT.Copy, scale=factors[:, a, j : j + 1]
+                        )
             nc.sync.dma_start(
-                out=out_view[:, a, HALF * half : HALF * (half + 1)], in_=o_sb[:].rearrange("p h d -> p (h d)")
+                out=out_view[:, first_tile : first_tile + tiles, first : first + width],
+                in_=o_sb[:].rearrange("p a h d -> p a (h d)"),
             )
 
         last_score_slot = FIRST_SCORE_SLOT + SCORE_TILES // TILES_A_SLOT - 1
-        first_attend = SLOTS + 1 - S_TILES
         v_ps = {}
+        v_bf = {}
         v_grouped = {}
-        inv_sums = {}
         for t in range(SLOTS + 1):
             after_scores = t - FIRST_SCORE_SLOT - HEAD_SLOTS - 2
             if t < PASSES:
@@ -444,22 +465,25 @@ def tile_bayesianattention_pa_k_kernel(
                 exponentials(TILES_A_SLOT * (t - 1 - FIRST_SCORE_SLOT))
             if FIRST_SCORE_SLOT <= t <= last_score_slot:
                 score_tiles(TILES_A_SLOT * (t - FIRST_SCORE_SLOT))
-            if t == first_attend - 2:
-                quantise_v(v_grouped[0], 0)
-                inv_sums[0] = invert_sums(0)
-            if t == last_score_slot + 2:
-                inv_sums[1] = invert_sums(1)
+            if t == EV["quant0"]:
+                quantise_v(0)
+                invert_sums(0)
+            if t == EV["group1"]:
+                group_v(1)
+            if t == EV["quant1"]:
+                quantise_v(1)
+                invert_sums(1)
+            if t == EV["inv2"]:
+                invert_sums(2)
             if t > 0:
-                half, g = divmod(t - 1, PASSES)
-                if g == 0:
-                    v_ps[half] = [
-                        v_psum.tile([P, HALF], F32, name="v_ps%d" % m, tag="v_ps%d" % m) for m in range(S_TILES)
-                    ]
-                project(v_ps[half], half, g)
-                if g == PASSES - 1:
-                    v_grouped[half] = group_v(round_v(v_ps[half]), half)
-            if t >= first_attend:
-                attend(inv_sums[0], 0, t - first_attend)
-        quantise_v(v_grouped[1], 1)
-        for a in range(S_TILES):
-            attend(inv_sums[1], 1, a)
+                project(t - 1)
+            if t == PASSES:
+                group_v(0)
+            if 0 <= t - EV["attend0"] < 4:
+                attend(0, t - EV["attend0"], (t - EV["attend0"]) % 2 == 0)
+            if 0 <= t - EV["attend1"] < 2:
+                attend(1, t - EV["attend1"], (t - EV["attend1"]) % 2 == 0)
+        group_v(2)
+        quantise_v(2)
+        attend(2, 0, True)
+        attend(2, 1, False)

@@ -32,7 +32,7 @@ HALVES = E // HALF
 HALF_HEADS = HALF // HD
 PLANES = 4
 STREAM_BUFS = 4
-QK_BEHIND = 6
+QK_BEHIND = 5
 W_BUFS = 5
 W_AHEAD = 3
 V_PARTS = ((0, 512), (512, 256), (768, 256))
@@ -45,8 +45,9 @@ EXP_PLAIN = 3
 
 SCORE_TILES = H * S_TILES
 SLOTS = HALVES * PASSES
-FIRST_SCORE_SLOT = 12
+FIRST_SCORE_SLOT = 11
 PREPARE_SLOTS = 2
+V_GROUP_SLOTS = (20, 22, 24, 26)
 TILES_A_SLOT = 2
 HEAD_SLOTS = S_TILES // TILES_A_SLOT
 
@@ -221,7 +222,6 @@ def tile_bayesianattention_pa_k_kernel(
                 scale=kappa[:, h : h + 1],
                 bias=neg_centre[:, h : h + 1],
             )
-        for h in range(H):
             nc.scalar.activation(
                 out=work[:, h, :],
                 in_=work[:, h, :],
@@ -385,11 +385,13 @@ def tile_bayesianattention_pa_k_kernel(
 
         def group_v(part):
             grouped = v_pool.tile([P, V_PARTS[part][1], S_TILES], BF16, align_bytes=64, name="v_grouped", bufs=2)
-            if part == 0:
-                scale_and_add(grouped[:], v_bf[part][:].rearrange("p m n -> p n m"), 1.0, 0.0)
-            else:
+            if part > 0:
                 nc.vector.tensor_copy(out=grouped[:], in_=v_bf[part][:].rearrange("p m n -> p n m"))
             v_grouped[part] = grouped
+
+        def group_head(i):
+            cols = slice(HD * i, HD * (i + 1))
+            nc.scalar.copy(out=v_grouped[0][:, cols, :], in_=v_bf[0][:, :, cols].rearrange("p m n -> p n m"))
 
         def quantise_v(part):
             first, width = V_PARTS[part]
@@ -465,6 +467,8 @@ def tile_bayesianattention_pa_k_kernel(
                 exponentials(TILES_A_SLOT * (t - 1 - FIRST_SCORE_SLOT))
             if FIRST_SCORE_SLOT <= t <= last_score_slot:
                 score_tiles(TILES_A_SLOT * (t - FIRST_SCORE_SLOT))
+            if t in V_GROUP_SLOTS:
+                group_head(V_GROUP_SLOTS.index(t))
             if t == EV["quant0"]:
                 quantise_v(0)
                 invert_sums(0)

from contextlib import ExitStack
import math

import concourse.mybir as mybir
from concourse.masks import make_identity

BF16 = mybir.dt.bfloat16
F32 = mybir.dt.float32
I32 = mybir.dt.int32
U32 = mybir.dt.uint32
U8 = mybir.dt.uint8
FP8X4 = mybir.dt.float8_e4m3fn_x4
ACT = mybir.ActivationFunctionType
ALU = mybir.AluOpType

P = 128
S = 512
D = 8192
H = 8
HD = 128
E = H * HD
EPS = 1e-5

S_TILES = S // P
K_PASS = 4 * P
PASSES = D // K_PASS
CHUNK_PASSES = 2
CHUNKS = PASSES // CHUNK_PASSES
CHUNK_K = CHUNK_PASSES * K_PASS
HALF = 512
HALVES = E // HALF
HALF_HEADS = HALF // HD
PLANES = 4
STREAM_BUFS = 4
QK_BEHIND = 5
W_BUFS = 5
W_AHEAD = 3
V_PARTS = ((0, 512), (512, 256), (768, 256))

PRIOR_W = S
CENTRE = math.log(64.0)
EXP_HALVINGS = 10
EXP_SERIES = (1.0, 1.0 / 2, 1.0 / 6, 1.0 / 24, 1.0 / 120)
EXP_PLAIN = 3

SCORE_TILES = H * S_TILES
SLOTS = HALVES * PASSES
FIRST_SCORE_SLOT = 11
PREPARE_SLOTS = 2
V_GROUP_SLOTS = (20, 22, 24, 26)
TILES_A_SLOT = 2
HEAD_SLOTS = S_TILES // TILES_A_SLOT

EV = {"quant0":27,"attend0":29,"group1":28,"quant1":29,"attend1":31,"inv2":30}

FLOPS = 2 * S * D * E + 2 * 2 * H * S * S * HD


def tile_bayesianattention_pa_k_kernel(
    tc, x, wv_words, wv_scales, q, k, mask, shape, scale, loc, out
):
    nc = tc.nc

    x_view = x.rearrange("b (u p r) k -> (b u) p r k", u=2, r=2)
    w_view = wv_words.rearrange("g p n t -> g p (n t)").bitcast(I32).rearrange("g p n -> p g n")
    w_scale_view = wv_scales.bitcast(I32)
    q_view = q.rearrange("b (a p) h d -> p (b a) (h d)", p=P)
    k_view = k.rearrange("b (a p) h d -> p (b a) (h d)", p=P)
    mask_view = mask.rearrange("b c (a p) j -> p (b c a) j", p=P)
    out_view = out.rearrange("b (a p) n -> p (b a) n", p=P)

    with ExitStack() as ctx:
        ctx.enter_context(tc.manual_schedule())
        keep = ctx.enter_context(tc.tile_pool(name="keep", bufs=1))
        stream = ctx.enter_context(tc.tile_pool(name="stream", bufs=STREAM_BUFS))
        w_pool = ctx.enter_context(tc.tile_pool(name="w_pool", bufs=W_BUFS))
        x_pool = ctx.enter_context(tc.tile_pool(name="x_pool", bufs=2))
        v_psum = ctx.enter_context(tc.psum_pool(name="v_psum", bufs=1))
        banks = ctx.enter_context(tc.psum_pool(name="banks", bufs=4))

        ident_bf = keep.tile([P, P], BF16)
        ident_f32 = keep.tile([P, P], F32)
        prior = keep.tile([P, H, PRIOR_W], F32)
        work = keep.tile([P, H, PRIOR_W], F32)
        mask_near = keep.tile([P, P], BF16)
        e_heads = [keep.tile([P, S_TILES, S], BF16, name="e_head%d" % i) for i in range(2)]
        e_grouped = [keep.tile([P, 4 * S], BF16, align_bytes=64, name="e_grouped%d" % i) for i in range(2)]
        qk_t = keep.tile([P, 2, H, S], BF16)
        row_sum = keep.tile([P, S_TILES, H], F32)
        w_planes = keep.tile([P, PASSES // PLANES, E], U8, align_bytes=64)
        x_codes = keep.tile([P, PASSES, S], U32, align_bytes=64)
        x_scales = keep.tile([P, PASSES, S], U8, align_bytes=64)
        e_codes = keep.tile([P, H, S], U32, align_bytes=64)
        e_scales = keep.tile([P, H, S], U8, align_bytes=64)
        v_codes = keep.tile([P, E], U32, align_bytes=64)
        v_scales = keep.tile([P, E], U8, align_bytes=64)
        inv_sum = keep.tile([P, S_TILES, H], F32)
        planes_words = w_planes[:].bitcast(I32)

        x_tiles = {}
        w_tiles = {}
        qk_rows = {}

        def load_x(c):
            x_sb = stream.tile([P, S_TILES, CHUNK_K], BF16, tag="stream", name="x_sb")
            for u in range(2):
                nc.sync.dma_start(
                    out=x_sb[:, 2 * u : 2 * u + 2, :], in_=x_view[u][:, :, CHUNK_K * c : CHUNK_K * (c + 1)]
                )
            x_tiles[c] = x_sb
            load_w(c)

        def load_rows(half):
            rows_sb = stream.tile([P, 2, S_TILES, HALF], BF16, tag="stream", name="rows_sb")
            for which in range(2):
                nc.sync.dma_start(
                    out=rows_sb[:, which, :, :], in_=(q_view, k_view)[which][:, :, HALF * half : HALF * (half + 1)]
                )
            qk_rows[half] = rows_sb

        def load_next(n):
            if n < QK_BEHIND:
                load_x(n)
            elif n == QK_BEHIND:
                load_rows(0)
            elif n < CHUNKS + 1:
                load_x(n - 1)
            elif n == CHUNKS + 1:
                load_rows(1)

        def load_w(i):
            part, c = divmod(i, CHUNKS)
            first, width = V_PARTS[part]
            first_pass = CHUNK_PASSES * c
            if part == 0 and first_pass % PLANES == 0:
                for j in range(4):
                    nc.sync.dma_start(
                        out=planes_words[32 * j : 32 * j + 4 * PLANES, first_pass // PLANES, :],
                        in_=w_scale_view[first_pass : first_pass + PLANES, 4 * j : 4 * j + 4, :],
                    )
            w_sb = w_pool.tile([P, CHUNK_PASSES, width], I32, align_bytes=64, name="w_sb")
            nc.sync.dma_start(out=w_sb[:], in_=w_view[:, first_pass : first_pass + CHUNK_PASSES, first : first + width])
            w_tiles[i] = w_sb

        nc.vector.memset(w_planes[:].rearrange("p t n -> p (t n)").bitcast(I32), 0)
        for i in range(2):
            nc.vector.memset(e_heads[i][:].rearrange("p a j -> p (a j)").bitcast(I32), 0)
            nc.vector.memset(e_grouped[i][:].bitcast(I32), 0)
        make_identity(nc, ident_f32[:])

        scale_bf = keep.tile([P, H], BF16)
        loc_bf = keep.tile([P, H], BF16)
        shape_bf = keep.tile([P, H], BF16)
        nc.sync.dma_start(out=scale_bf[:], in_=scale.rearrange("a h b c -> (a h b c)").partition_broadcast(P))
        nc.sync.dma_start(out=loc_bf[:], in_=loc.rearrange("a h b c -> (a h b c)").partition_broadcast(P))
        nc.sync.dma_start(out=shape_bf[:], in_=shape.rearrange("a h b c -> (a h b c)").partition_broadcast(P))
        for n in range(STREAM_BUFS):
            load_next(n)
        nc.sync.dma_start(out=mask_near[:], in_=mask_view[:, 0, 0:P])


        kappa = keep.tile([P, H], F32)
        neg_centre = keep.tile([P, H], F32)
        eps_col = keep.tile([P, 1], F32)
        nc.vector.memset(eps_col[:], EPS)
        nc.vector.tensor_scalar_add(out=kappa[:], in0=shape_bf[:], scalar1=-1.0)
        nc.vector.tensor_scalar_mul(out=neg_centre[:], in0=kappa[:], scalar1=-CENTRE)
        slope = keep.tile([P, H], F32)
        exp_loc = keep.tile([P, H], F32)
        exp_neg_loc = keep.tile([P, H], F32)
        lift = keep.tile([P, H], F32)
        nc.scalar.activation(out=exp_loc[:], in_=loc_bf[:], func=ACT.Exp)
        nc.scalar.activation(out=exp_neg_loc[:], in_=loc_bf[:], func=ACT.Exp, scale=-1.0)
        nc.scalar.activation(out=slope[:], in_=scale_bf[:], func=ACT.Exp)
        nc.scalar.activation(out=lift[:], in_=kappa[:], func=ACT.Exp, scale=CENTRE)
        neg_offset = keep.tile([P, H], F32)
        eps_lift = keep.tile([P, H], F32)
        nc.vector.tensor_sub(out=neg_offset[:], in0=exp_neg_loc[:], in1=exp_loc[:])
        nc.vector.tensor_scalar_mul(out=eps_lift[:], in0=lift[:], scalar1=EPS)

        dist_i = keep.tile([P, PRIOR_W], I32)
        dist = keep.tile([P, PRIOR_W], F32)
        nc.gpsimd.iota(dist_i[:], pattern=[[1, PRIOR_W]], base=-(S - P), channel_multiplier=-1)
        nc.vector.tensor_copy(out=dist[:], in_=dist_i[:])

        small = keep.tile([P, H], F32)
        grown = keep.tile([P, H], F32)
        plus = keep.tile([P, H], F32)
        nc.gpsimd.tensor_scalar(
            out=plus[:], in0=shape_bf[:], scalar1=CENTRE, scalar2=-CENTRE, op0=ALU.mult, op1=ALU.add
        )
        nc.gpsimd.tensor_tensor(out=small[:], in0=plus[:], in1=scale_bf[:], op=ALU.add)

        def scale_and_add(out, in0, factor, term):
            nc.gpsimd.tensor_scalar(out=out, in0=in0, scalar1=factor, scalar2=term, op0=ALU.mult, op1=ALU.add)

        scale_and_add(small[:], small[:], 1.0 / 2**EXP_HALVINGS, 0.0)
        scale_and_add(grown[:], small[:], EXP_SERIES[-1], 0.0)
        for coefficient in reversed(EXP_SERIES[:-1]):
            scale_and_add(plus[:], grown[:], 1.0, coefficient)
            nc.gpsimd.tensor_tensor(out=grown[:], in0=plus[:], in1=small[:], op=ALU.mult)
        for squaring in range(EXP_HALVINGS - EXP_PLAIN):
            scale_and_add(plus[:], grown[:], 1.0, 2.0)
            nc.gpsimd.tensor_tensor(out=grown[:], in0=plus[:], in1=grown[:], op=ALU.mult)
        scale_and_add(grown[:], grown[:], 1.0, 1.0)
        for squaring in range(EXP_PLAIN):
            nc.gpsimd.tensor_tensor(out=grown[:], in0=grown[:], in1=grown[:], op=ALU.mult)
        slope_lift = grown
        make_identity(nc, ident_bf[:])

        for h in range(H):
            nc.scalar.activation(out=work[:, h, :], in_=dist[:], func=ACT.Abs, bias=neg_offset[:, h : h + 1])
        for h in range(H):
            nc.scalar.activation(
                out=prior[:, h, :], in_=work[:, h, :], func=ACT.Ln, scale=slope[:, h : h + 1], bias=eps_col[:, 0:1]
            )
        for h in range(H):
            nc.scalar.activation(
                out=prior[:, h, :],
                in_=prior[:, h, :],
                func=ACT.Exp,
                scale=kappa[:, h : h + 1],
                bias=neg_centre[:, h : h + 1],
            )
            nc.scalar.activation(
                out=work[:, h, :],
                in_=work[:, h, :],
                func=ACT.Identity,
                scale=slope_lift[:, h : h + 1],
                bias=eps_lift[:, h : h + 1],
            )

        def finish_tables(heads):
            for h in heads:
                nc.vector.tensor_mul(out=prior[:, h, :], in0=prior[:, h, :], in1=work[:, h, :])
            for h in heads:
                nc.vector.tensor_sub(out=prior[:, h, S - P : S], in0=prior[:, h, S - P : S], in1=mask_near[:])

        v_pool = ctx.enter_context(tc.tile_pool(name="v_pool", bufs=1))
        o_pool = ctx.enter_context(tc.tile_pool(name="o_pool", bufs=4))
        score_pool = ctx.enter_context(tc.tile_pool(name="score_pool", bufs=4))

        neg_s = {}
        neg_max = {}

        def transpose_rows(half, which):
            for pair in range(HALF_HEADS // 2):
                qk_ps = banks.tile([P, 2, S], BF16, tag="bank")
                for i in range(2):
                    head = slice(HD * (2 * pair + i), HD * (2 * pair + i + 1))
                    for a in range(S_TILES):
                        nc.tensor.transpose(
                            qk_ps[:, i, P * a : P * (a + 1)], qk_rows[half][:, which, a, head], ident_bf[:]
                        )
                first_head = HALF_HEADS * half + 2 * pair
                nc.scalar.copy(out=qk_t[:, which, first_head : first_head + 2, :], in_=qk_ps[:])

        def transpose_x(g):
            c, local = divmod(g, CHUNK_PASSES)
            x_words = x_tiles[c][:].bitcast(F32)
            grouped = x_pool.tile([P, 4 * S], BF16, align_bytes=64, name="x_grouped")
            grouped_words = grouped[:].bitcast(F32).rearrange("p (s w) -> p s w", w=2)
            first = (K_PASS // 2) * local
            for b in range(S_TILES // 2):
                xt_ps = banks.tile([P, 2, 2 * P], F32, tag="bank")
                for m in range(2):
                    for w in range(2):
                        nc.tensor.transpose(
                            xt_ps[:, w, P * m : P * (m + 1)],
                            x_words[:, 2 * b + m, first + w : first + K_PASS // 2 : 2],
                            ident_f32[:],
                        )
                side_by_side = grouped_words[:, 2 * P * b : 2 * P * (b + 1), :]
                if g >= FIRST_SCORE_SLOT - PREPARE_SLOTS:
                    nc.scalar.copy(out=side_by_side, in_=xt_ps[:].rearrange("p w s -> p s w"))
                else:
                    nc.vector.tensor_copy(out=side_by_side, in_=xt_ps[:].rearrange("p w s -> p s w"))
            nc.vector.quantize_mx(out=x_codes[:, g, :].bitcast(FP8X4), scales=x_scales[:, g, :], in_=grouped[:])
            if local == CHUNK_PASSES - 1:
                load_next(c + STREAM_BUFS)

        def project(u):
            if u < PASSES:
                part, passes = 0, [u]
            else:
                part, c = 1 + (u - PASSES) // CHUNKS, (u - PASSES) % CHUNKS
                passes = [CHUNK_PASSES * c, CHUNK_PASSES * c + 1]
            first, width = V_PARTS[part]
            if passes[0] == 0:
                v_ps[part] = [
                    v_psum.tile([P, width], F32, name="v_ps%d" % m, tag="v_ps%d" % m) for m in range(S_TILES)
                ]
            for g in passes:
                c, local = divmod(g, CHUNK_PASSES)
                i = CHUNKS * part + c
                plane = PLANES * (g % PLANES)
                for m in range(S_TILES):
                    cols = slice(P * m, P * (m + 1))
                    nc.tensor.matmul_mx(
                        out=v_ps[part][m][:],
                        lhsT=x_codes[:, g, cols].bitcast(FP8X4),
                        lhsT_scale=x_scales[:, g, cols],
                        rhs=w_tiles[i][:, local, :].bitcast(FP8X4),
                        rhs_scale=w_planes[plane:P, g // PLANES, first : first + width],
                        start=(g == 0),
                        stop=(g == PASSES - 1),
                    )
                if local == CHUNK_PASSES - 1 and CHUNKS <= i + W_AHEAD < len(V_PARTS) * CHUNKS:
                    load_w(i + W_AHEAD)
            if passes[-1] == PASSES - 1:
                round_v(part)

        def score_tiles(first_tile):
            tiles = [divmod(n, S_TILES) for n in range(first_tile, first_tile + TILES_A_SLOT)]
            s_ps = {}
            for h, a in tiles:
                s_ps[a] = banks.tile([P, S], F32, tag="bank", name="s_ps")
                nc.tensor.matmul(
                    s_ps[a][:, 0 : P * (a + 1)],
                    lhsT=qk_t[:, 0, h, P * a : P * (a + 1)],
                    rhs=qk_t[:, 1, h, 0 : P * (a + 1)],
                    start=True,
                    stop=True,
                )
            for h, a in tiles:
                neg_s[a] = score_pool.tile([P, S], F32, name="neg_s")
                nc.vector.scalar_tensor_tensor(
                    out=neg_s[a][:, 0 : P * (a + 1)],
                    in0=s_ps[a][:, 0 : P * (a + 1)],
                    scalar=-1.0 / math.sqrt(HD),
                    in1=prior[:, h, S - P * (a + 1) : S],
                    op0=ALU.mult,
                    op1=ALU.add,
                )
            for h, a in tiles:
                neg_max[a] = score_pool.tile([P, 1], F32, name="neg_max")
                nc.vector.tensor_scalar(
                    out=neg_s[a][:, 0 : P * (a + 1)],
                    in0=neg_s[a][:, 0 : P * (a + 1)],
                    scalar1=1.0,
                    scalar2=None,
                    op0=ALU.mult,
                    op1=ALU.min,
                    accum_out=neg_max[a][:],
                )

        def exponentials(first_tile):
            for h, a in [divmod(n, S_TILES) for n in range(first_tile, first_tile + TILES_A_SLOT)]:
                nc.scalar.activation(
                    out=e_heads[h % 2][:, a, 0 : P * (a + 1)],
                    in_=neg_s[a][:, 0 : P * (a + 1)],
                    func=ACT.Exp,
                    scale=-1.0,
                    bias=neg_max[a][:, 0:1],
                    accum_out=row_sum[:, a, h : h + 1],
                )

        def transpose_e(h):
            e_words = e_heads[h % 2][:].bitcast(F32)
            grouped_words = e_grouped[h % 2][:].bitcast(F32).rearrange("p (i u) -> p i u", u=2)
            low_ps = banks.tile([P, 2 * P], F32, tag="bank")
            for a in range(2):
                nc.tensor.transpose(low_ps[:, P * a : P * (a + 1)], e_words[:, a, 0:P], ident_f32[:])
            nc.scalar.copy(out=grouped_words[:, 0 : 2 * P, 0], in_=low_ps[:])
            high_ps = banks.tile([P, 2, 2 * P], F32, tag="bank")
            for a in range(2, S_TILES):
                for u in range(2):
                    nc.tensor.transpose(
                        high_ps[:, u, P * (a - 2) : P * (a - 1)], e_words[:, a, P * u : P * (u + 1)], ident_f32[:]
                    )
            nc.scalar.copy(out=grouped_words[:, 2 * P : 4 * P, :], in_=high_ps[:].rearrange("p u i -> p i u"))

        def quantise_e(h):
            nc.vector.quantize_mx(
                out=e_codes[:, h, :].bitcast(FP8X4), scales=e_scales[:, h, :], in_=e_grouped[h % 2][:]
            )

        def round_v(part):
            v_bf[part] = v_pool.tile([P, S_TILES, V_PARTS[part][1]], BF16, name="v_bf", bufs=2)
            for m in range(S_TILES):
                if m % 2 == 0:
                    nc.scalar.copy(out=v_bf[part][:, m, :], in_=v_ps[part][m][:])
                else:
                    nc.vector.tensor_copy(out=v_bf[part][:, m, :], in_=v_ps[part][m][:])

        def group_v(part):
            grouped = v_pool.tile([P, V_PARTS[part][1], S_TILES], BF16, align_bytes=64, name="v_grouped", bufs=2)
            if part > 0:
                nc.vector.tensor_copy(out=grouped[:], in_=v_bf[part][:].rearrange("p m n -> p n m"))
            v_grouped[part] = grouped

        def group_head(i):
            cols = slice(HD * i, HD * (i + 1))
            nc.scalar.copy(out=v_grouped[0][:, cols, :], in_=v_bf[0][:, :, cols].rearrange("p m n -> p n m"))

        def quantise_v(part):
            first, width = V_PARTS[part]
            nc.vector.quantize_mx(
                out=v_codes[:, first : first + width].bitcast(FP8X4),
                scales=v_scales[:, first : first + width],
                in_=v_grouped[part][:].rearrange("p n m -> p (n m)"),
            )

        def invert_sums(part):
            first, width = V_PARTS[part]
            heads = slice(first // HD, (first + width) // HD)
            nc.vector.reciprocal(out=inv_sum[:, :, heads], in_=row_sum[:, :, heads])

        def attend(part, i, on_vector):
            first, width = V_PARTS[part]
            heads = width // HD
            tiles = HALF // width
            first_head = first // HD
            first_tile = tiles * i
            o_ps = banks.tile([P, tiles, heads, HD], F32, tag="bank")
            for a in range(tiles):
                rows = slice(P * (first_tile + a), P * (first_tile + a + 1))
                for j in range(heads):
                    h = first_head + j
                    cols = slice(HD * h, HD * (h + 1))
                    nc.tensor.matmul_mx(
                        out=o_ps[:, a, j, :],
                        lhsT=e_codes[:, h, rows].bitcast(FP8X4),
                        lhsT_scale=e_scales[:, h, rows],
                        rhs=v_codes[:, cols].bitcast(FP8X4),
                        rhs_scale=v_scales[:, cols],
                        start=True,
                        stop=True,
                    )
            o_sb = o_pool.tile([P, tiles, heads, HD], F32)
            factors = inv_sum[:, first_tile : first_tile + tiles, first_head : first_head + heads]
            if on_vector:
                nc.vector.tensor_tensor(
                    out=o_sb[:], in0=o_ps[:], in1=factors.unsqueeze(3).to_broadcast([P, tiles, heads, HD]), op=ALU.mult
                )
            else:
                for a in range(tiles):
                    for j in range(heads):
                        nc.scalar.activation(
                            out=o_sb[:, a, j, :], in_=o_ps[:, a, j, :], func=ACT.Copy, scale=factors[:, a, j : j + 1]
                        )
            nc.sync.dma_start(
                out=out_view[:, first_tile : first_tile + tiles, first : first + width],
                in_=o_sb[:].rearrange("p a h d -> p a (h d)"),
            )

        last_score_slot = FIRST_SCORE_SLOT + SCORE_TILES // TILES_A_SLOT - 1
        v_ps = {}
        v_bf = {}
        v_grouped = {}
        for t in range(SLOTS + 1):
            after_scores = t - FIRST_SCORE_SLOT - HEAD_SLOTS - 2
            if t < PASSES:
                transpose_x(t)
            prepare = t - (FIRST_SCORE_SLOT - PREPARE_SLOTS)
            if 0 <= prepare < PREPARE_SLOTS:
                transpose_rows(0, prepare)
                finish_tables(range(H // PREPARE_SLOTS * prepare, H // PREPARE_SLOTS * (prepare + 1)))
            prepare_late = prepare - HALF_HEADS * HEAD_SLOTS
            if 0 <= prepare_late < PREPARE_SLOTS:
                transpose_rows(1, prepare_late)
            if after_scores >= 0 and after_scores % HEAD_SLOTS == 0 and after_scores // HEAD_SLOTS < H:
                transpose_e(after_scores // HEAD_SLOTS)
            if after_scores >= 1 and after_scores % HEAD_SLOTS == 1 and after_scores // HEAD_SLOTS < H:
                quantise_e(after_scores // HEAD_SLOTS)
            if FIRST_SCORE_SLOT < t <= last_score_slot + 1:
                exponentials(TILES_A_SLOT * (t - 1 - FIRST_SCORE_SLOT))
            if FIRST_SCORE_SLOT <= t <= last_score_slot:
                score_tiles(TILES_A_SLOT * (t - FIRST_SCORE_SLOT))
            if t in V_GROUP_SLOTS:
                group_head(V_GROUP_SLOTS.index(t))
            if t == EV["quant0"]:
                quantise_v(0)
                invert_sums(0)
            if t == EV["group1"]:
                group_v(1)
            if t == EV["quant1"]:
                quantise_v(1)
                invert_sums(1)
            if t == EV["inv2"]:
                invert_sums(2)
            if t > 0:
                project(t - 1)
            if t == PASSES:
                group_v(0)
            if 0 <= t - EV["attend0"] < 4:
                attend(0, t - EV["attend0"], (t - EV["attend0"]) % 2 == 0)
            if 0 <= t - EV["attend1"] < 2:
                attend(1, t - EV["attend1"], (t - EV["attend1"]) % 2 == 0)
        group_v(2)
        quantise_v(2)
        attend(2, 0, True)
        attend(2, 1, False)
